import numpy as np
import ml_dtypes


def mxq(x, axis, fmt="e4m3"):
    dtype, down = {"e4m3": (ml_dtypes.float8_e4m3fn, 7), "e5m2": (ml_dtypes.float8_e5m2, 14)}[fmt]
    v = np.moveaxis(np.asarray(x, np.float32).astype(ml_dtypes.bfloat16).astype(np.float64), axis, -1)
    blocks = v.reshape(v.shape[:-1] + (-1, 32))
    amax = np.abs(blocks).max(-1, keepdims=True)
    byte = np.maximum(np.where(amax > 0, np.frexp(amax)[1] - 1 + 127, 0) - down, 1)
    scale = np.exp2(byte - 127.0)
    codes = (blocks / scale).astype(np.float32).astype(dtype).astype(np.float64)
    return np.moveaxis((codes * scale).reshape(v.shape), -1, axis)


WIDE = False


def mx_kscale(k):
    if not WIDE:
        return np.ones(k)
    levels = np.array([10, -10, 5, -5, 0])
    if k % 512:
        return np.exp2(np.random.permutation(np.resize(levels, k // 32))).repeat(32)
    a = np.empty((k // 512, 16))
    for p in range(k // 512):
        a[p, :8] = np.random.permutation(np.resize(levels, 8))
        for g in range(8):
            far = levels[np.abs(levels - a[p, g]) >= 10]
            a[p, g + 8] = far[np.random.randint(len(far))]
    return np.exp2(a.ravel()).repeat(32)


BF16 = ml_dtypes.bfloat16


def bf(x):
    return np.asarray(x, np.float32).astype(BF16)


def f64(x):
    return np.asarray(x).astype(np.float64)


T, D, H, C = 8192, 512, 4, 32
E = H * C
EPS = 1e-6
BASE = 10000.0


def rope_tables():
    inv_freq = 1.0 / BASE ** (np.arange(0, C, 2) / C)
    freqs = np.arange(T)[:, None] * inv_freq[None, :]
    return np.sin(freqs), np.cos(freqs)


def rotate_every_two(v):
    return np.stack((-v[..., 1::2], v[..., ::2]), axis=-1).reshape(v.shape)


def apply_rope(v, sin, cos):
    sin = np.repeat(sin, 2, axis=-1)[None]
    cos = np.repeat(cos, 2, axis=-1)[None]
    return v * cos + rotate_every_two(v) * sin


def layernorm(v, w):
    mu = v.mean(-1, keepdims=True)
    var = v.var(-1, keepdims=True)
    return (v - mu) / np.sqrt(var + EPS) * w


def heads(v):
    return v.reshape(T, H, C).transpose(1, 0, 2)


def setup_inputs():
    s = mx_kscale(D)
    return {"x": bf(np.random.standard_normal((T, D)) * s),
            "W_attn": bf(np.random.standard_normal((3 * E, D)) / np.sqrt(D) / s[None, :]),
            "b_attn": bf(np.random.standard_normal(3 * E) * 0.3),
            "q_ln_w": bf(1.0 + 0.2 * np.random.standard_normal(C)),
            "k_ln_w": bf(1.0 + 0.2 * np.random.standard_normal(C))}


def reference(x, W_attn, b_attn, q_ln_w, k_ln_w):
    xq = mxq(f64(x), 1, "e4m3")
    wq, wk, wv = np.split(f64(W_attn), 3, axis=0)
    bq, bk, bv = np.split(f64(b_attn), 3)
    q = heads((xq @ mxq(wq, 1, "e4m3").T) + bq)
    k = heads((xq @ mxq(wk, 1, "e4m3").T) + bk)
    v = heads((xq @ mxq(wv, 1, "e4m3").T) + bv)
    q = layernorm(q, f64(q_ln_w))
    k = layernorm(k, f64(k_ln_w))
    sin, cos = rope_tables()
    return apply_rope(q, sin, cos), apply_rope(k, sin, cos), v

@@ -1,0 +1,365 @@
+from contextlib import ExitStack
+
+import concourse.mybir as mybir
+from concourse.masks import make_identity
+
+F32 = mybir.dt.float32
+BF16 = mybir.dt.bfloat16
+I32 = mybir.dt.int32
+U32 = mybir.dt.uint32
+U8 = mybir.dt.uint8
+FP8X4 = mybir.dt.float8_e4m3fn_x4
+ALU = mybir.AluOpType
+ACT = mybir.ActivationFunctionType
+
+T, D, H, C = 8192, 512, 4, 32
+E = H * C
+EPS = 1e-6
+BASE = 10000.0
+PI = 3.141592653589793
+
+P = 128
+SUB = 8
+CHUNK = P * SUB
+CHUNKS = T // CHUNK
+POS = CHUNKS * SUB
+PAIRS = C // 2
+GROUPS = 2 * H * SUB
+X_BUFS = 6
+ROUND = 12582912.0
+
+FLOPS = 2 * T * D * 3 * E
+
+
+def split_frequency(pair):
+    turns = BASE ** (-pair / PAIRS) / (2.0 * PI)
+    scale = 1.0
+    while turns * scale < 1024.0:
+        scale = scale * 2.0
+    high = round(turns * scale) / scale
+    return high, turns - high
+
+
+def tile_causalselfattention_pa_t_kernel(
+    tc, x, W_attn, b_attn, q_ln_w, k_ln_w, out_0, out_1, out_2
+):
+    nc = tc.nc
+    with ExitStack() as ctx:
+        const = ctx.enter_context(tc.tile_pool(name="const", bufs=1))
+        setup = ctx.enter_context(tc.tile_pool(name="setup", bufs=1))
+        xpool = ctx.enter_context(tc.tile_pool(name="xpool", bufs=X_BUFS))
+        quant = ctx.enter_context(tc.tile_pool(name="quant", bufs=2))
+        work = ctx.enter_context(tc.tile_pool(name="work", bufs=2))
+        small = ctx.enter_context(tc.tile_pool(name="small", bufs=2))
+        ps_t = ctx.enter_context(tc.psum_pool(name="ps_t", bufs=2))
+        ps_qk = ctx.enter_context(tc.psum_pool(name="ps_qk", bufs=4))
+        ps_v = ctx.enter_context(tc.psum_pool(name="ps_v", bufs=2))
+        ctx.enter_context(tc.manual_schedule())
+
+        x_rows = {}
+        grouped = {}
+        codes = {}
+        scales = {}
+        acc_qk = {}
+        acc_v = {}
+        u_qk = {}
+        stats = {}
+        std = {}
+        rstd = {}
+        shift = {}
+        straight = {}
+        crossed = {}
+
+        def load(g):
+            x_rows[g] = xpool.tile([P, SUB, D], BF16, name="x_rows")
+            nc.sync.dma_start(
+                out=x_rows[g][:],
+                in_=x[g * CHUNK : (g + 1) * CHUNK, :].rearrange("(p s) k -> p s k", s=SUB),
+            )
+
+        def turn(g):
+            grouped[g] = quant.tile([P, CHUNK * 4], BF16, align_bytes=64, name="grouped")
+            words = grouped[g][:].bitcast(F32).rearrange("p (s m u) -> p s m u", s=SUB, u=2)
+            for b in range(SUB // 2):
+                xt = ps_t.tile([P, 2, 2, P], F32, tag="xt")
+                for s in range(2):
+                    for u in range(2):
+                        nc.tensor.transpose(
+                            xt[:, s, u, :],
+                            x_rows[g][:, 2 * b + s, :].bitcast(F32)[:, u : 2 * P : 2],
+                            ident[:],
+                        )
+                nc.scalar.copy(
+                    out=words[:, 2 * b : 2 * b + 2, :, :],
+                    in_=xt[:].rearrange("p s u m -> p s m u"),
+                )
+            if g + X_BUFS < CHUNKS:
+                load(g + X_BUFS)
+
+        load(0)
+        w_rows = setup.tile([P, 3, D], BF16)
+        nc.sync.dma_start(out=w_rows[:], in_=W_attn.rearrange("(a p) k -> p a k", p=P))
+        for g in range(1, X_BUFS):
+            load(g)
+        vectors = setup.tile([P, 4 * E], BF16)
+        nc.vector.memset(vectors[:], 0.0)
+        nc.scalar.dma_start(out=vectors[0:1, 0 : 3 * E], in_=b_attn.rearrange("(o n) -> o n", o=1))
+        nc.scalar.dma_start(
+            out=vectors[0:1, 3 * E : 3 * E + C], in_=q_ln_w.rearrange("(o n) -> o n", o=1)
+        )
+        nc.scalar.dma_start(
+            out=vectors[0:1, 3 * E + C : 3 * E + 2 * C], in_=k_ln_w.rearrange("(o n) -> o n", o=1)
+        )
+        ones = setup.tile([P, P], BF16)
+        nc.vector.memset(ones[:], 1.0)
+        eps = const.tile([P, 1], F32)
+        nc.vector.memset(eps[:], EPS)
+        ident = const.tile([P, P], F32)
+        make_identity(nc, ident[:])
+        pos_i = setup.tile([P, POS], I32)
+        nc.gpsimd.iota(pos_i[:], pattern=[[CHUNK, CHUNKS], [1, SUB]], base=0, channel_multiplier=SUB)
+
+        pos = setup.tile([P, POS], F32)
+        nc.vector.tensor_copy(out=pos[:], in_=pos_i[:])
+        whole = setup.tile([P, PAIRS, POS], F32)
+        for j in range(PAIRS):
+            high, low = split_frequency(j)
+            nc.vector.tensor_scalar(
+                out=whole[:, j, :], in0=pos[:], scalar1=high, scalar2=ROUND,
+                op0=ALU.mult, op1=ALU.add,
+            )
+        nc.vector.tensor_scalar_sub(out=whole[:], in0=whole[:], scalar1=ROUND)
+        turns = setup.tile([P, 2, PAIRS, POS], F32)
+        for j in range(PAIRS):
+            high, low = split_frequency(j)
+            nc.vector.scalar_tensor_tensor(
+                out=whole[:, j, :], in0=pos[:], scalar=high, in1=whole[:, j, :],
+                op0=ALU.mult, op1=ALU.subtract,
+            )
+            nc.vector.scalar_tensor_tensor(
+                out=turns[:, 0, j, :], in0=pos[:], scalar=low, in1=whole[:, j, :],
+                op0=ALU.mult, op1=ALU.add,
+            )
+        nc.vector.tensor_scalar_add(out=turns[:, 1, :, :], in0=turns[:, 0, :, :], scalar1=0.25)
+        nearest = setup.tile([P, 2, PAIRS, POS], F32)
+        nc.vector.tensor_scalar(
+            out=nearest[:], in0=turns[:], scalar1=ROUND, scalar2=ROUND,
+            op0=ALU.add, op1=ALU.subtract,
+        )
+        nc.vector.tensor_sub(out=turns[:], in0=turns[:], in1=nearest[:])
+        turn(0)
+        trig = setup.tile([P, 2, POS, PAIRS], F32)
+        for s in range(2):
+            nc.scalar.activation(
+                out=trig[:, s, :, :], in_=turns[:, s, :, :].rearrange("p j i -> p i j"),
+                func=ACT.Sin, scale=2.0 * PI,
+            )
+
+        w_grouped = setup.tile([P, 3 * E * 4], BF16, align_bytes=64)
+        w_words = w_grouped[:].bitcast(F32).rearrange("p (a r u) -> p a r u", a=3, u=2)
+        w_codes = const.tile([P, 3 * E], U32, align_bytes=64)
+        w_scales = const.tile([P, 3 * E], U8, align_bytes=64)
+        for a in range(3):
+            wt = ps_t.tile([P, 2, 2, P], F32, tag="xt")
+            for u in range(2):
+                nc.tensor.transpose(
+                    wt[:, 0, u, :], w_rows[:, a, :].bitcast(F32)[:, u : 2 * P : 2], ident[:]
+                )
+            if a < 2:
+                for e in range(2):
+                    nc.vector.tensor_copy(
+                        out=w_words[:, a, :, :].rearrange("p (h e j) u -> p h e j u", h=H, e=2)[
+                            :, :, e, :, :
+                        ],
+                        in_=wt[:, 0, :, :].rearrange("p u (h j e) -> p h e j u", h=H, e=2)[
+                            :, :, e, :, :
+                        ],
+                    )
+            else:
+                nc.vector.tensor_copy(
+                    out=w_words[:, a, :, :], in_=wt[:, 0, :, :].rearrange("p u r -> p r u")
+                )
+        nc.vector.quantize_mx(
+            out=w_codes[:, 0 : 2 * E].bitcast(FP8X4),
+            scales=w_scales[:, 0 : 2 * E],
+            in_=w_grouped[:, 0 : 2 * E * 4],
+        )
+        nc.vector.quantize_mx(
+            out=w_codes[:, 2 * E : 3 * E].bitcast(FP8X4),
+            scales=w_scales[:, 2 * E : 3 * E],
+            in_=w_grouped[:, 2 * E * 4 : 3 * E * 4],
+        )
+
+        spread = ps_qk.tile([P, 4 * E], F32, tag="acc")
+        nc.tensor.matmul(out=spread[:], lhsT=ones[:], rhs=vectors[:], start=True, stop=True)
+        bias = const.tile([P, 3 * E], F32)
+        nc.vector.tensor_copy(
+            out=bias[:, 0 : 2 * E].rearrange("p (g e j) -> p g e j", e=2, j=PAIRS),
+            in_=spread[:, 0 : 2 * E].rearrange("p (g j e) -> p g e j", e=2, j=PAIRS),
+        )
+        nc.vector.tensor_copy(out=bias[:, 2 * E : 3 * E], in_=spread[:, 2 * E : 3 * E])
+        gain = const.tile([P, 2, 2, PAIRS], F32)
+        nc.vector.tensor_copy(
+            out=gain[:],
+            in_=spread[:, 3 * E : 3 * E + 2 * C].rearrange("p (t j e) -> p t e j", t=2, e=2),
+        )
+        cross = const.tile([P, 2, 2, PAIRS], F32)
+        nc.vector.tensor_scalar_mul(out=cross[:, :, 0, :], in0=gain[:, :, 1, :], scalar1=-1.0)
+        nc.vector.tensor_copy(out=cross[:, :, 1, :], in_=gain[:, :, 0, :])
+
+        own = const.tile([P, 2, POS, 2, PAIRS], F32)
+        other = const.tile([P, 2, 2, POS, PAIRS], F32)
+        for t in range(2):
+            for e in range(2):
+                nc.gpsimd.tensor_mul(
+                    out=other[:, e, t, :, :],
+                    in0=trig[:, 0, :, :],
+                    in1=cross[:, t, e, :].unsqueeze(1).to_broadcast([P, POS, PAIRS]),
+                )
+            nc.gpsimd.tensor_mul(
+                out=own[:, t, :, :, :],
+                in0=trig[:, 1, :, :].unsqueeze(2).to_broadcast([P, POS, 2, PAIRS]),
+                in1=gain[:, t, :, :].unsqueeze(1).to_broadcast([P, POS, 2, PAIRS]),
+            )
+
+        def project(g):
+            codes[g] = quant.tile([P, CHUNK], U32, align_bytes=64, name="codes")
+            scales[g] = quant.tile([P, CHUNK], U8, align_bytes=64, name="scales")
+            nc.vector.quantize_mx(
+                out=codes[g][:].bitcast(FP8X4), scales=scales[g][:], in_=grouped[g][:]
+            )
+            acc_qk[g] = []
+            for b in range(SUB // 2):
+                acc = ps_qk.tile([P, 2, 2 * E], F32, tag="acc")
+                for s in range(2):
+                    cols = slice((2 * b + s) * P, (2 * b + s + 1) * P)
+                    nc.tensor.matmul_mx(
+                        out=acc[:, s, :],
+                        lhsT=codes[g][:, cols].bitcast(FP8X4), lhsT_scale=scales[g][:, cols],
+                        rhs=w_codes[:, 0 : 2 * E].bitcast(FP8X4), rhs_scale=w_scales[:, 0 : 2 * E],
+                        start=True, stop=True,
+                    )
+                acc_qk[g].append(acc)
+            acc_v[g] = []
+            for b in range(SUB // 4):
+                acc = ps_v.tile([P, 4, E], F32, tag="acc_v")
+                for s in range(4):
+                    cols = slice((4 * b + s) * P, (4 * b + s + 1) * P)
+                    nc.tensor.matmul_mx(
+                        out=acc[:, s, :],
+                        lhsT=codes[g][:, cols].bitcast(FP8X4), lhsT_scale=scales[g][:, cols],
+                        rhs=w_codes[:, 2 * E : 3 * E].bitcast(FP8X4),
+                        rhs_scale=w_scales[:, 2 * E : 3 * E],
+                        start=True, stop=True,
+                    )
+                acc_v[g].append(acc)
+
+        def add_bias(g):
+            u_qk[g] = work.tile([P, 2 * H, SUB, C], F32, name="u_qk")
+            for b in range(SUB // 2):
+                nc.vector.tensor_add(
+                    out=u_qk[g][:, :, 2 * b : 2 * b + 2, :],
+                    in0=acc_qk[g][b][:].rearrange("p s (g c) -> p g s c", c=C),
+                    in1=bias[:, 0 : 2 * E].rearrange("p (g c) -> p g c", c=C).unsqueeze(2)
+                    .to_broadcast([P, 2 * H, 2, C]),
+                )
+            v_out = work.tile([P, H, SUB, C], F32)
+            for b in range(SUB // 4):
+                nc.vector.tensor_add(
+                    out=v_out[:, :, 4 * b : 4 * b + 4, :],
+                    in0=acc_v[g][b][:].rearrange("p s (h c) -> p h s c", c=C),
+                    in1=bias[:, 2 * E : 3 * E].rearrange("p (h c) -> p h c", c=C).unsqueeze(2)
+                    .to_broadcast([P, H, 4, C]),
+                )
+            nc.sync.dma_start(
+                out=out_2[:, g * CHUNK : (g + 1) * CHUNK, :].rearrange(
+                    "h (p s) c -> p h (s c)", s=SUB
+                ),
+                in_=v_out[:].rearrange("p h s c -> p h (s c)"),
+            )
+
+        def measure(g):
+            pairs_of_groups = u_qk[g][:].rearrange("p g s c -> p (g s) c").rearrange(
+                "p (n two) c -> p n c two", two=2
+            )
+            stats[g] = small.tile([P, GROUPS, 3], F32, name="stats")
+            for n in range(GROUPS // 2):
+                nc.vector.bn_stats(
+                    out=stats[g][:, 2 * n : 2 * n + 2, :].rearrange("p two k -> p (two k)"),
+                    in_=pairs_of_groups[:, n, :, :],
+                )
+            std[g] = small.tile([P, GROUPS], F32, name="std")
+            nc.scalar.activation(
+                out=std[g][:], in_=stats[g][:, :, 2], func=ACT.Sqrt, scale=1.0 / C, bias=eps[:]
+            )
+
+        def invert(g):
+            rstd[g] = small.tile([P, GROUPS], F32, name="rstd")
+            nc.vector.reciprocal(out=rstd[g][:], in_=std[g][:])
+            shift[g] = small.tile([P, GROUPS], F32, name="shift")
+            nc.vector.scalar_tensor_tensor(
+                out=shift[g][:], in0=stats[g][:, :, 1], scalar=-1.0, in1=rstd[g][:],
+                op0=ALU.mult, op1=ALU.mult,
+            )
+
+        def normalise(g):
+            groups = u_qk[g][:].rearrange("p g s c -> p (g s) c")
+            for i in range(GROUPS):
+                nc.scalar.activation(
+                    out=groups[:, i, :], in_=groups[:, i, :], func=ACT.Identity,
+                    scale=rstd[g][:, i : i + 1], bias=shift[g][:, i : i + 1],
+                )
+
+        def rotate_partner(g):
+            normed = u_qk[g][:].rearrange("p g s (e j) -> p (g s) e j", e=2)
+            crossed[g] = work.tile([P, GROUPS, 2, PAIRS], F32, name="crossed")
+            for e in range(2):
+                nc.gpsimd.tensor_mul(
+                    out=crossed[g][:, :, e, :].rearrange("p (t h s) j -> p t h s j", t=2, h=H),
+                    in0=normed[:, :, 1 - e, :].rearrange("p (t h s) j -> p t h s j", t=2, h=H),
+                    in1=other[:, e, :, g * SUB : (g + 1) * SUB, :].unsqueeze(2)
+                    .to_broadcast([P, 2, H, SUB, PAIRS]),
+                )
+
+        def rotate_own(g):
+            straight[g] = work.tile([P, GROUPS, 2, PAIRS], F32, name="straight")
+            nc.vector.tensor_mul(
+                out=straight[g][:].rearrange("p (t h s) e j -> p t h (s e j)", t=2, h=H),
+                in0=u_qk[g][:].rearrange("p (t h) s c -> p t h (s c)", t=2),
+                in1=own[:, :, g * SUB : (g + 1) * SUB, :, :].rearrange("p t s e j -> p t (s e j)")
+                .unsqueeze(2).to_broadcast([P, 2, H, SUB * C]),
+            )
+
+        def finish(g):
+            qk_out = work.tile([P, GROUPS, PAIRS, 2], F32)
+            nc.vector.tensor_add(
+                out=qk_out[:],
+                in0=straight[g][:].rearrange("p i e j -> p i j e"),
+                in1=crossed[g][:].rearrange("p i e j -> p i j e"),
+            )
+            for t, dest in enumerate((out_0, out_1)):
+                nc.sync.dma_start(
+                    out=dest[:, g * CHUNK : (g + 1) * CHUNK, :].rearrange(
+                        "h (p s) c -> p h (s c)", s=SUB
+                    ),
+                    in_=qk_out[:, t * H * SUB : (t + 1) * H * SUB, :, :].rearrange(
+                        "p (h s) j e -> p h (s j e)", h=H
+                    ),
+                )
+
+        for i in range(-1, CHUNKS + 1):
+            if 0 <= i - 1:
+                rotate_partner(i - 1)
+            if i + 2 < CHUNKS:
+                turn(i + 2)
+            if 0 <= i < CHUNKS:
+                add_bias(i)
+                measure(i)
+            if i + 1 < CHUNKS:
+                project(i + 1)
+            if 0 <= i < CHUNKS:
+                invert(i)
+                normalise(i)
+            if 0 <= i - 1:
+                rotate_own(i - 1)
+                finish(i - 1)

@@ -19,13 +19,14 @@ BASE = 10000.0
 PI = 3.141592653589793
 
 P = 128
-SUB = 8
-CHUNK = P * SUB
-CHUNKS = T // CHUNK
-POS = CHUNKS * SUB
+SUB = 4
+UNIT = P * SUB
+UNITS = T // UNIT
+POS = UNITS * SUB
 PAIRS = C // 2
-GROUPS = 2 * H * SUB
-X_BUFS = 6
+GROUPS = 2 * SUB * H
+PIECE = 16
+PIECES = POS // PIECE
 ROUND = 12582912.0
 
 FLOPS = 2 * T * D * 3 * E
@@ -46,62 +47,44 @@ def tile_causalselfattention_pa_t_kernel(
     nc = tc.nc
     with ExitStack() as ctx:
         const = ctx.enter_context(tc.tile_pool(name="const", bufs=1))
-        setup = ctx.enter_context(tc.tile_pool(name="setup", bufs=1))
-        xpool = ctx.enter_context(tc.tile_pool(name="xpool", bufs=X_BUFS))
-        quant = ctx.enter_context(tc.tile_pool(name="quant", bufs=2))
-        work = ctx.enter_context(tc.tile_pool(name="work", bufs=2))
-        small = ctx.enter_context(tc.tile_pool(name="small", bufs=2))
-        ps_t = ctx.enter_context(tc.psum_pool(name="ps_t", bufs=2))
-        ps_qk = ctx.enter_context(tc.psum_pool(name="ps_qk", bufs=4))
-        ps_v = ctx.enter_context(tc.psum_pool(name="ps_v", bufs=2))
+        xpool = ctx.enter_context(tc.tile_pool(name="xpool", bufs=UNITS))
+        two = ctx.enter_context(tc.tile_pool(name="two", bufs=2))
+        three = ctx.enter_context(tc.tile_pool(name="three", bufs=3))
+        ps_x = ctx.enter_context(tc.psum_pool(name="ps_x", bufs=2))
+        ps_c = ctx.enter_context(tc.psum_pool(name="ps_c", bufs=2))
+        ps_v = ctx.enter_context(tc.psum_pool(name="ps_v", bufs=1))
+        ps_t = ctx.enter_context(tc.psum_pool(name="ps_t", bufs=3))
         ctx.enter_context(tc.manual_schedule())
 
         x_rows = {}
+        x_turned = {}
         grouped = {}
         codes = {}
         scales = {}
-        acc_qk = {}
-        acc_v = {}
-        u_qk = {}
+        acc = {}
+        biased = {}
+        u = {}
         stats = {}
         std = {}
         rstd = {}
         shift = {}
+        normed = {}
         straight = {}
         crossed = {}
 
-        def load(g):
-            x_rows[g] = xpool.tile([P, SUB, D], BF16, name="x_rows")
+        def load(i):
+            x_rows[i] = xpool.tile([P, SUB, D], BF16, name="x_rows")
             nc.sync.dma_start(
-                out=x_rows[g][:],
-                in_=x[g * CHUNK : (g + 1) * CHUNK, :].rearrange("(p s) k -> p s k", s=SUB),
+                out=x_rows[i][:],
+                in_=x[i * UNIT : (i + 1) * UNIT, :].rearrange("(p s) k -> p s k", s=SUB),
             )
 
-        def turn(g):
-            grouped[g] = quant.tile([P, CHUNK * 4], BF16, align_bytes=64, name="grouped")
-            words = grouped[g][:].bitcast(F32).rearrange("p (s m u) -> p s m u", s=SUB, u=2)
-            for b in range(SUB // 2):
-                xt = ps_t.tile([P, 2, 2, P], F32, tag="xt")
-                for s in range(2):
-                    for u in range(2):
-                        nc.tensor.transpose(
-                            xt[:, s, u, :],
-                            x_rows[g][:, 2 * b + s, :].bitcast(F32)[:, u : 2 * P : 2],
-                            ident[:],
-                        )
-                nc.scalar.copy(
-                    out=words[:, 2 * b : 2 * b + 2, :, :],
-                    in_=xt[:].rearrange("p s u m -> p s m u"),
-                )
-            if g + X_BUFS < CHUNKS:
-                load(g + X_BUFS)
-
         load(0)
-        w_rows = setup.tile([P, 3, D], BF16)
+        w_rows = const.tile([P, 3, D], BF16)
         nc.sync.dma_start(out=w_rows[:], in_=W_attn.rearrange("(a p) k -> p a k", p=P))
-        for g in range(1, X_BUFS):
-            load(g)
-        vectors = setup.tile([P, 4 * E], BF16)
+        for i in range(1, UNITS):
+            load(i)
+        vectors = const.tile([P, 4 * E], BF16)
         nc.vector.memset(vectors[:], 0.0)
         nc.scalar.dma_start(out=vectors[0:1, 0 : 3 * E], in_=b_attn.rearrange("(o n) -> o n", o=1))
         nc.scalar.dma_start(
@@ -110,18 +93,22 @@ def tile_causalselfattention_pa_t_kernel(
         nc.scalar.dma_start(
             out=vectors[0:1, 3 * E + C : 3 * E + 2 * C], in_=k_ln_w.rearrange("(o n) -> o n", o=1)
         )
-        ones = setup.tile([P, P], BF16)
+        ones = const.tile([P, P], BF16)
         nc.vector.memset(ones[:], 1.0)
         eps = const.tile([P, 1], F32)
         nc.vector.memset(eps[:], EPS)
+        zero = const.tile([P, 1], F32)
+        nc.vector.memset(zero[:], 0.0)
+        unused = const.tile([P, 1], F32)
+        nc.scalar.activation(out=unused[:], in_=zero[:], func=ACT.Sin)
         ident = const.tile([P, P], F32)
         make_identity(nc, ident[:])
-        pos_i = setup.tile([P, POS], I32)
-        nc.gpsimd.iota(pos_i[:], pattern=[[CHUNK, CHUNKS], [1, SUB]], base=0, channel_multiplier=SUB)
+        pos_i = const.tile([P, POS], I32)
+        nc.gpsimd.iota(pos_i[:], pattern=[[UNIT, UNITS], [1, SUB]], base=0, channel_multiplier=SUB)
 
-        pos = setup.tile([P, POS], F32)
+        pos = const.tile([P, POS], F32)
         nc.vector.tensor_copy(out=pos[:], in_=pos_i[:])
-        whole = setup.tile([P, PAIRS, POS], F32)
+        whole = const.tile([P, PAIRS, POS], F32)
         for j in range(PAIRS):
             high, low = split_frequency(j)
             nc.vector.tensor_scalar(
@@ -129,237 +116,317 @@ def tile_causalselfattention_pa_t_kernel(
                 op0=ALU.mult, op1=ALU.add,
             )
         nc.vector.tensor_scalar_sub(out=whole[:], in0=whole[:], scalar1=ROUND)
-        turns = setup.tile([P, 2, PAIRS, POS], F32)
+        angle = const.tile([P, PAIRS, POS], F32)
         for j in range(PAIRS):
             high, low = split_frequency(j)
             nc.vector.scalar_tensor_tensor(
                 out=whole[:, j, :], in0=pos[:], scalar=high, in1=whole[:, j, :],
                 op0=ALU.mult, op1=ALU.subtract,
             )
+        for j in range(PAIRS):
+            high, low = split_frequency(j)
             nc.vector.scalar_tensor_tensor(
-                out=turns[:, 0, j, :], in0=pos[:], scalar=low, in1=whole[:, j, :],
+                out=angle[:, j, :], in0=pos[:], scalar=low, in1=whole[:, j, :],
                 op0=ALU.mult, op1=ALU.add,
             )
-        nc.vector.tensor_scalar_add(out=turns[:, 1, :, :], in0=turns[:, 0, :, :], scalar1=0.25)
-        nearest = setup.tile([P, 2, PAIRS, POS], F32)
-        nc.vector.tensor_scalar(
-            out=nearest[:], in0=turns[:], scalar1=ROUND, scalar2=ROUND,
-            op0=ALU.add, op1=ALU.subtract,
-        )
-        nc.vector.tensor_sub(out=turns[:], in0=turns[:], in1=nearest[:])
-        turn(0)
-        trig = setup.tile([P, 2, POS, PAIRS], F32)
-        for s in range(2):
-            nc.scalar.activation(
-                out=trig[:, s, :, :], in_=turns[:, s, :, :].rearrange("p j i -> p i j"),
-                func=ACT.Sin, scale=2.0 * PI,
-            )
 
-        w_grouped = setup.tile([P, 3 * E * 4], BF16, align_bytes=64)
-        w_words = w_grouped[:].bitcast(F32).rearrange("p (a r u) -> p a r u", a=3, u=2)
-        w_codes = const.tile([P, 3 * E], U32, align_bytes=64)
-        w_scales = const.tile([P, 3 * E], U8, align_bytes=64)
-        for a in range(3):
-            wt = ps_t.tile([P, 2, 2, P], F32, tag="xt")
-            for u in range(2):
-                nc.tensor.transpose(
-                    wt[:, 0, u, :], w_rows[:, a, :].bitcast(F32)[:, u : 2 * P : 2], ident[:]
-                )
-            if a < 2:
-                for e in range(2):
-                    nc.vector.tensor_copy(
-                        out=w_words[:, a, :, :].rearrange("p (h e j) u -> p h e j u", h=H, e=2)[
-                            :, :, e, :, :
-                        ],
-                        in_=wt[:, 0, :, :].rearrange("p u (h j e) -> p h e j u", h=H, e=2)[
-                            :, :, e, :, :
-                        ],
-                    )
-            else:
-                nc.vector.tensor_copy(
-                    out=w_words[:, a, :, :], in_=wt[:, 0, :, :].rearrange("p u r -> p r u")
-                )
-        nc.vector.quantize_mx(
-            out=w_codes[:, 0 : 2 * E].bitcast(FP8X4),
-            scales=w_scales[:, 0 : 2 * E],
-            in_=w_grouped[:, 0 : 2 * E * 4],
-        )
-        nc.vector.quantize_mx(
-            out=w_codes[:, 2 * E : 3 * E].bitcast(FP8X4),
-            scales=w_scales[:, 2 * E : 3 * E],
-            in_=w_grouped[:, 2 * E * 4 : 3 * E * 4],
-        )
-
-        spread = ps_qk.tile([P, 4 * E], F32, tag="acc")
-        nc.tensor.matmul(out=spread[:], lhsT=ones[:], rhs=vectors[:], start=True, stop=True)
-        bias = const.tile([P, 3 * E], F32)
-        nc.vector.tensor_copy(
-            out=bias[:, 0 : 2 * E].rearrange("p (g e j) -> p g e j", e=2, j=PAIRS),
-            in_=spread[:, 0 : 2 * E].rearrange("p (g j e) -> p g e j", e=2, j=PAIRS),
-        )
-        nc.vector.tensor_copy(out=bias[:, 2 * E : 3 * E], in_=spread[:, 2 * E : 3 * E])
-        gain = const.tile([P, 2, 2, PAIRS], F32)
-        nc.vector.tensor_copy(
-            out=gain[:],
-            in_=spread[:, 3 * E : 3 * E + 2 * C].rearrange("p (t j e) -> p t e j", t=2, e=2),
-        )
-        cross = const.tile([P, 2, 2, PAIRS], F32)
-        nc.vector.tensor_scalar_mul(out=cross[:, :, 0, :], in0=gain[:, :, 1, :], scalar1=-1.0)
-        nc.vector.tensor_copy(out=cross[:, :, 1, :], in_=gain[:, :, 0, :])
-
-        own = const.tile([P, 2, POS, 2, PAIRS], F32)
-        other = const.tile([P, 2, 2, POS, PAIRS], F32)
-        for t in range(2):
-            for e in range(2):
-                nc.gpsimd.tensor_mul(
-                    out=other[:, e, t, :, :],
-                    in0=trig[:, 0, :, :],
-                    in1=cross[:, t, e, :].unsqueeze(1).to_broadcast([P, POS, PAIRS]),
-                )
-            nc.gpsimd.tensor_mul(
-                out=own[:, t, :, :, :],
-                in0=trig[:, 1, :, :].unsqueeze(2).to_broadcast([P, POS, 2, PAIRS]),
-                in1=gain[:, t, :, :].unsqueeze(1).to_broadcast([P, POS, 2, PAIRS]),
-            )
-
-        def project(g):
-            codes[g] = quant.tile([P, CHUNK], U32, align_bytes=64, name="codes")
-            scales[g] = quant.tile([P, CHUNK], U8, align_bytes=64, name="scales")
-            nc.vector.quantize_mx(
-                out=codes[g][:].bitcast(FP8X4), scales=scales[g][:], in_=grouped[g][:]
-            )
-            acc_qk[g] = []
+        def turn(i):
+            x_turned[i] = []
             for b in range(SUB // 2):
-                acc = ps_qk.tile([P, 2, 2 * E], F32, tag="acc")
+                xt = ps_x.tile([P, 2, 2, P], F32, tag="xt")
                 for s in range(2):
-                    cols = slice((2 * b + s) * P, (2 * b + s + 1) * P)
-                    nc.tensor.matmul_mx(
-                        out=acc[:, s, :],
-                        lhsT=codes[g][:, cols].bitcast(FP8X4), lhsT_scale=scales[g][:, cols],
-                        rhs=w_codes[:, 0 : 2 * E].bitcast(FP8X4), rhs_scale=w_scales[:, 0 : 2 * E],
-                        start=True, stop=True,
-                    )
-                acc_qk[g].append(acc)
-            acc_v[g] = []
-            for b in range(SUB // 4):
-                acc = ps_v.tile([P, 4, E], F32, tag="acc_v")
-                for s in range(4):
-                    cols = slice((4 * b + s) * P, (4 * b + s + 1) * P)
-                    nc.tensor.matmul_mx(
-                        out=acc[:, s, :],
-                        lhsT=codes[g][:, cols].bitcast(FP8X4), lhsT_scale=scales[g][:, cols],
-                        rhs=w_codes[:, 2 * E : 3 * E].bitcast(FP8X4),
-                        rhs_scale=w_scales[:, 2 * E : 3 * E],
-                        start=True, stop=True,
-                    )
-                acc_v[g].append(acc)
+                    for half in range(2):
+                        nc.tensor.transpose(
+                            xt[:, s, half, :],
+                            x_rows[i][:, 2 * b + s, :].bitcast(F32)[:, half : 2 * P : 2],
+                            ident[:],
+                        )
+                x_turned[i].append(xt)
+            grouped[i] = two.tile([P, UNIT * 4], BF16, align_bytes=64, name="grouped")
 
-        def add_bias(g):
-            u_qk[g] = work.tile([P, 2 * H, SUB, C], F32, name="u_qk")
-            for b in range(SUB // 2):
-                nc.vector.tensor_add(
-                    out=u_qk[g][:, :, 2 * b : 2 * b + 2, :],
-                    in0=acc_qk[g][b][:].rearrange("p s (g c) -> p g s c", c=C),
-                    in1=bias[:, 0 : 2 * E].rearrange("p (g c) -> p g c", c=C).unsqueeze(2)
-                    .to_broadcast([P, 2 * H, 2, C]),
+        def regroup(i, b):
+            words = grouped[i][:].bitcast(F32).rearrange("p (s m e) -> p s m e", s=SUB, e=2)
+            nc.scalar.copy(
+                out=words[:, 2 * b : 2 * b + 2, :, :],
+                in_=x_turned[i][b][:].rearrange("p s e m -> p s m e"),
+            )
+
+        def quantise(i):
+            codes[i] = two.tile([P, UNIT], U32, align_bytes=64, name="codes")
+            scales[i] = two.tile([P, UNIT], U8, align_bytes=64, name="scales")
+            nc.vector.quantize_mx(
+                out=codes[i][:].bitcast(FP8X4), scales=scales[i][:], in_=grouped[i][:]
+            )
+
+        def project(i):
+            acc[i] = []
+            for t in range(2):
+                cm = ps_c.tile([P, UNIT], F32, tag="cm")
+                nc.tensor.matmul_mx(
+                    out=cm[:],
+                    lhsT=w_codes[:, t * E : (t + 1) * E].bitcast(FP8X4),
+                    lhsT_scale=w_scales[:, t * E : (t + 1) * E],
+                    rhs=codes[i][:].bitcast(FP8X4), rhs_scale=scales[i][:],
+                    start=True, stop=True,
                 )
-            v_out = work.tile([P, H, SUB, C], F32)
-            for b in range(SUB // 4):
-                nc.vector.tensor_add(
-                    out=v_out[:, :, 4 * b : 4 * b + 4, :],
-                    in0=acc_v[g][b][:].rearrange("p s (h c) -> p h s c", c=C),
-                    in1=bias[:, 2 * E : 3 * E].rearrange("p (h c) -> p h c", c=C).unsqueeze(2)
-                    .to_broadcast([P, H, 4, C]),
+                acc[i].append(cm)
+            av = ps_v.tile([P, SUB, E], F32, tag="av")
+            for s in range(SUB):
+                cols = slice(s * P, (s + 1) * P)
+                nc.tensor.matmul_mx(
+                    out=av[:, s, :],
+                    lhsT=codes[i][:, cols].bitcast(FP8X4), lhsT_scale=scales[i][:, cols],
+                    rhs=w_codes[:, 2 * E : 3 * E].bitcast(FP8X4),
+                    rhs_scale=w_scales[:, 2 * E : 3 * E],
+                    start=True, stop=True,
                 )
+            acc[i].append(av)
+
+        def add_bias(i):
+            biased[i] = []
+            for t in range(2):
+                cb = two.tile([P, UNIT], F32, tag="cb" + str(t))
+                nc.scalar.activation(
+                    out=cb[:], in_=acc[i][t][:], func=ACT.Identity, bias=bias_qk[:, t : t + 1]
+                )
+                biased[i].append(cb)
+
+        def turn_back(i):
+            u[i] = []
+            for t in range(2):
+                tm = ps_t.tile([P, SUB, E], F32, tag="tm")
+                for s in range(SUB):
+                    nc.tensor.transpose(
+                        tm[:, s, :], biased[i][t][:, s * P : (s + 1) * P], ident[:]
+                    )
+                u[i].append(tm)
+
+        def finish_v(i):
+            v_out = three.tile([P, H, SUB, C], F32)
+            nc.vector.tensor_add(
+                out=v_out[:],
+                in0=acc[i][2][:].rearrange("p s (h c) -> p h s c", c=C),
+                in1=bias_v[:].rearrange("p (h c) -> p h c", c=C).unsqueeze(2)
+                .to_broadcast([P, H, SUB, C]),
+            )
             nc.sync.dma_start(
-                out=out_2[:, g * CHUNK : (g + 1) * CHUNK, :].rearrange(
+                out=out_2[:, i * UNIT : (i + 1) * UNIT, :].rearrange(
                     "h (p s) c -> p h (s c)", s=SUB
                 ),
                 in_=v_out[:].rearrange("p h s c -> p h (s c)"),
             )
 
-        def measure(g):
-            pairs_of_groups = u_qk[g][:].rearrange("p g s c -> p (g s) c").rearrange(
-                "p (n two) c -> p n c two", two=2
-            )
-            stats[g] = small.tile([P, GROUPS, 3], F32, name="stats")
-            for n in range(GROUPS // 2):
-                nc.vector.bn_stats(
-                    out=stats[g][:, 2 * n : 2 * n + 2, :].rearrange("p two k -> p (two k)"),
-                    in_=pairs_of_groups[:, n, :, :],
-                )
-            std[g] = small.tile([P, GROUPS], F32, name="std")
+        def measure(i):
+            stats[i] = three.tile([P, GROUPS, 3], F32, name="stats")
+            for t in range(2):
+                for s in range(SUB):
+                    for h in range(0, H, 2):
+                        g = (t * SUB + s) * H + h
+                        nc.vector.bn_stats(
+                            out=stats[i][:, g : g + 2, :].rearrange("p two k -> p (two k)"),
+                            in_=u[i][t][:, s, h * C : (h + 2) * C].rearrange(
+                                "p (two c) -> p c two", two=2
+                            ),
+                        )
+
+        def root(i):
+            std[i] = three.tile([P, GROUPS], F32, name="std")
             nc.scalar.activation(
-                out=std[g][:], in_=stats[g][:, :, 2], func=ACT.Sqrt, scale=1.0 / C, bias=eps[:]
+                out=std[i][:], in_=stats[i][:, :, 2], func=ACT.Sqrt, scale=1.0 / C, bias=eps[:]
             )
 
-        def invert(g):
-            rstd[g] = small.tile([P, GROUPS], F32, name="rstd")
-            nc.vector.reciprocal(out=rstd[g][:], in_=std[g][:])
-            shift[g] = small.tile([P, GROUPS], F32, name="shift")
+        def invert(i):
+            rstd[i] = three.tile([P, GROUPS], F32, name="rstd")
+            nc.vector.reciprocal(out=rstd[i][:], in_=std[i][:])
+
+        def offset(i):
+            shift[i] = three.tile([P, GROUPS], F32, name="shift")
             nc.vector.scalar_tensor_tensor(
-                out=shift[g][:], in0=stats[g][:, :, 1], scalar=-1.0, in1=rstd[g][:],
+                out=shift[i][:], in0=stats[i][:, :, 1], scalar=-1.0, in1=rstd[i][:],
                 op0=ALU.mult, op1=ALU.mult,
             )
 
-        def normalise(g):
-            groups = u_qk[g][:].rearrange("p g s c -> p (g s) c")
-            for i in range(GROUPS):
-                nc.scalar.activation(
-                    out=groups[:, i, :], in_=groups[:, i, :], func=ACT.Identity,
-                    scale=rstd[g][:, i : i + 1], bias=shift[g][:, i : i + 1],
-                )
+        def normalise(i):
+            normed[i] = three.tile([P, 2, H, SUB, C], F32, name="normed")
+            for t in range(2):
+                for s in range(SUB):
+                    for h in range(H):
+                        g = (t * SUB + s) * H + h
+                        nc.scalar.activation(
+                            out=normed[i][:, t, h, s, :],
+                            in_=u[i][t][:, s, h * C : (h + 1) * C], func=ACT.Identity,
+                            scale=rstd[i][:, g : g + 1], bias=shift[i][:, g : g + 1],
+                        )
 
-        def rotate_partner(g):
-            normed = u_qk[g][:].rearrange("p g s (e j) -> p (g s) e j", e=2)
-            crossed[g] = work.tile([P, GROUPS, 2, PAIRS], F32, name="crossed")
-            for e in range(2):
+        def times_sine(i):
+            crossed[i] = two.tile([P, 2, H, SUB * C], F32, name="crossed")
+            for t in range(2):
                 nc.gpsimd.tensor_mul(
-                    out=crossed[g][:, :, e, :].rearrange("p (t h s) j -> p t h s j", t=2, h=H),
-                    in0=normed[:, :, 1 - e, :].rearrange("p (t h s) j -> p t h s j", t=2, h=H),
-                    in1=other[:, e, :, g * SUB : (g + 1) * SUB, :].unsqueeze(2)
-                    .to_broadcast([P, 2, H, SUB, PAIRS]),
+                    out=crossed[i][:, t, :, :],
+                    in0=normed[i][:, t, :, :, :].rearrange("p h s c -> p h (s c)"),
+                    in1=of_unit(sine, i)[:, t, :, :].rearrange("p s c -> p (s c)")
+                    .unsqueeze(1).to_broadcast([P, H, SUB * C]),
                 )
 
-        def rotate_own(g):
-            straight[g] = work.tile([P, GROUPS, 2, PAIRS], F32, name="straight")
+        def times_cosine(i):
+            straight[i] = two.tile([P, 2, H, SUB * C], F32, name="straight")
             nc.vector.tensor_mul(
-                out=straight[g][:].rearrange("p (t h s) e j -> p t h (s e j)", t=2, h=H),
-                in0=u_qk[g][:].rearrange("p (t h) s c -> p t h (s c)", t=2),
-                in1=own[:, :, g * SUB : (g + 1) * SUB, :, :].rearrange("p t s e j -> p t (s e j)")
+                out=straight[i][:],
+                in0=normed[i][:].rearrange("p t h s c -> p t h (s c)"),
+                in1=of_unit(cosine, i).rearrange("p t s c -> p t (s c)")
                 .unsqueeze(2).to_broadcast([P, 2, H, SUB * C]),
             )
 
-        def finish(g):
-            qk_out = work.tile([P, GROUPS, PAIRS, 2], F32)
+        def finish_qk(i):
+            qk_out = three.tile([P, 2, H, SUB * C], F32)
             nc.vector.tensor_add(
-                out=qk_out[:],
-                in0=straight[g][:].rearrange("p i e j -> p i j e"),
-                in1=crossed[g][:].rearrange("p i e j -> p i j e"),
+                out=qk_out[:].rearrange("p t h (n e) -> p (t h n) e", e=2),
+                in0=straight[i][:].rearrange("p t h (n e) -> p (t h n) e", e=2),
+                in1=crossed[i][:].rearrange("p t h (n e) -> p (t h n) e", e=2)[:, :, ::-1],
             )
             for t, dest in enumerate((out_0, out_1)):
                 nc.sync.dma_start(
-                    out=dest[:, g * CHUNK : (g + 1) * CHUNK, :].rearrange(
+                    out=dest[:, i * UNIT : (i + 1) * UNIT, :].rearrange(
                         "h (p s) c -> p h (s c)", s=SUB
                     ),
-                    in_=qk_out[:, t * H * SUB : (t + 1) * H * SUB, :, :].rearrange(
-                        "p (h s) j e -> p h (s j e)", h=H
-                    ),
+                    in_=qk_out[:, t, :, :],
                 )
 
-        for i in range(-1, CHUNKS + 1):
-            if 0 <= i - 1:
-                rotate_partner(i - 1)
-            if i + 2 < CHUNKS:
-                turn(i + 2)
-            if 0 <= i < CHUNKS:
-                add_bias(i)
-                measure(i)
-            if i + 1 < CHUNKS:
-                project(i + 1)
-            if 0 <= i < CHUNKS:
-                invert(i)
-                normalise(i)
-            if 0 <= i - 1:
-                rotate_own(i - 1)
-                finish(i - 1)
+        turn(0)
+        w_grouped = const.tile([P, 3 * E * 4], BF16, align_bytes=64)
+        w_words = w_grouped[:].bitcast(F32).rearrange("p (a r e) -> p a r e", a=3, e=2)
+        w_codes = const.tile([P, 3 * E], U32, align_bytes=64)
+        w_scales = const.tile([P, 3 * E], U8, align_bytes=64)
+        for a in range(3):
+            wt = ps_t.tile([P, SUB, E], F32, tag="tm")
+            for half in range(2):
+                nc.tensor.transpose(
+                    wt[:, half, :], w_rows[:, a, :].bitcast(F32)[:, half : 2 * P : 2], ident[:]
+                )
+            nc.vector.tensor_copy(
+                out=w_words[:, a, :, :], in_=wt[:, 0:2, :].rearrange("p e r -> p r e")
+            )
+        for b in range(SUB // 2):
+            regroup(0, b)
+        nc.vector.quantize_mx(
+            out=w_codes[:, 0 : 2 * E].bitcast(FP8X4), scales=w_scales[:, 0 : 2 * E],
+            in_=w_grouped[:, 0 : 2 * E * 4],
+        )
+        nc.vector.quantize_mx(
+            out=w_codes[:, 2 * E : 3 * E].bitcast(FP8X4), scales=w_scales[:, 2 * E : 3 * E],
+            in_=w_grouped[:, 2 * E * 4 : 3 * E * 4],
+        )
+
+        spread = ps_v.tile([P, SUB, E], F32, tag="av")
+        nc.tensor.matmul(
+            out=spread[:, 0:2, :].rearrange("p s c -> p (s c)"), lhsT=ones[:],
+            rhs=vectors[:, 2 * E : 4 * E], start=True, stop=True,
+        )
+        for t in range(2):
+            nc.tensor.matmul(
+                out=spread[:, 2 + t, :], lhsT=vectors[:, t * E : (t + 1) * E], rhs=ones[:],
+                start=True, stop=True,
+            )
+        bias_qk = const.tile([P, 2], F32)
+        nc.vector.tensor_copy(out=bias_qk[:], in_=spread[:, 2:4, 0])
+        bias_v = const.tile([P, E], F32)
+        nc.vector.tensor_copy(out=bias_v[:], in_=spread[:, 0, :])
+        gain = const.tile([P, 2, PAIRS, 2], F32)
+        nc.vector.tensor_copy(
+            out=gain[:].rearrange("p t j e -> p (t j e)"), in_=spread[:, 1, 0 : 2 * C]
+        )
+        signed = const.tile([P, 2, PAIRS, 2], F32)
+        nc.vector.tensor_copy(out=signed[:, :, :, 0], in_=gain[:, :, :, 0])
+        nc.vector.tensor_scalar_mul(out=signed[:, :, :, 1], in0=gain[:, :, :, 1], scalar1=-1.0)
+        quantise(0)
+
+        turns = {}
+        trig = {}
+        cosine = {}
+        sine = {}
+
+        def reduce_turns(n):
+            here = angle[:, :, n * PIECE : (n + 1) * PIECE]
+            turns[n] = const.tile([P, 2, PAIRS, PIECE], F32, name="turns" + str(n))
+            nearest = const.tile([P, 2, PAIRS, PIECE], F32, name="nearest" + str(n))
+            nc.vector.tensor_scalar_add(out=turns[n][:, 1, :, :], in0=here, scalar1=0.25)
+            nc.vector.tensor_scalar(
+                out=nearest[:, 0, :, :], in0=here, scalar1=ROUND, scalar2=ROUND,
+                op0=ALU.add, op1=ALU.subtract,
+            )
+            nc.vector.tensor_scalar(
+                out=nearest[:, 1, :, :], in0=turns[n][:, 1, :, :], scalar1=ROUND, scalar2=ROUND,
+                op0=ALU.add, op1=ALU.subtract,
+            )
+            nc.vector.tensor_sub(out=turns[n][:, 0, :, :], in0=here, in1=nearest[:, 0, :, :])
+            nc.vector.tensor_sub(
+                out=turns[n][:, 1, :, :], in0=turns[n][:, 1, :, :], in1=nearest[:, 1, :, :]
+            )
+
+        def waves(n):
+            trig[n] = const.tile([P, 2, PIECE, PAIRS], F32, name="trig" + str(n))
+            nc.scalar.activation(
+                out=trig[n][:], in_=turns[n][:].rearrange("p w j i -> p w i j"),
+                func=ACT.Sin, scale=2.0 * PI,
+            )
+
+        def fold(n, part):
+            t = part % 2
+            if part == 0:
+                cosine[n] = const.tile([P, 2, PIECE, C], F32, name="cosine" + str(n))
+                sine[n] = const.tile([P, 2, PIECE, C], F32, name="sine" + str(n))
+            table, wave, factor = ((cosine, 1, gain), (sine, 0, signed))[part // 2]
+            nc.gpsimd.tensor_mul(
+                out=table[n][:, t, :, :].rearrange("p i (j e) -> p i j e", e=2),
+                in0=trig[n][:, wave, :, :].unsqueeze(3).to_broadcast([P, PIECE, PAIRS, 2]),
+                in1=factor[:, t, :, :].unsqueeze(1).to_broadcast([P, PIECE, PAIRS, 2]),
+            )
+
+        def of_unit(table, i):
+            first = i * SUB % PIECE
+            return table[i * SUB // PIECE][:, :, first : first + SUB, :]
+
+        def live(i):
+            return 0 <= i < UNITS
+
+        for n in range(UNITS + 4):
+            if live(n - 2):
+                turn_back(n - 2)
+            if live(n - 4):
+                times_sine(n - 4)
+            if live(n) and n > 0:
+                turn(n)
+            if live(n - 2):
+                finish_v(n - 2)
+                measure(n - 2)
+            if live(n - 3):
+                normalise(n - 3)
+            if live(n - 1) and n > 1:
+                quantise(n - 1)
+            if live(n) and n > 0:
+                regroup(n, 0)
+            if live(n - 2):
+                root(n - 2)
+            if live(n) and n > 0:
+                regroup(n, 1)
+            if live(n - 1):
+                project(n - 1)
+            if live(n - 2):
+                invert(n - 2)
+            if live(n - 3):
+                times_cosine(n - 3)
+            if live(n - 2):
+                offset(n - 2)
+            if live(n - 4):
+                finish_qk(n - 4)
+            if live(n - 1):
+                add_bias(n - 1)
+            if n == 1:
+                for piece in range(PIECES):
+                    reduce_turns(piece)
+                    waves(piece)
+                nc.scalar.activation(out=unused[:], in_=zero[:], func=ACT.Sqrt)
+                for part in range(4):
+                    fold(0, part)
+            if n >= 3 and n < 3 + 4 * (PIECES - 1):
+                fold((n + 1) // 4, (n + 1) % 4)

@@ -376,7 +376,7 @@ def tile_causalselfattention_pa_t_kernel(
                 cosine[n] = const.tile([P, 2, PIECE, C], F32, name="cosine" + str(n))
                 sine[n] = const.tile([P, 2, PIECE, C], F32, name="sine" + str(n))
             table, wave, factor = ((cosine, 1, gain), (sine, 0, signed))[part // 2]
-            nc.gpsimd.tensor_mul(
+            nc.vector.tensor_mul(
                 out=table[n][:, t, :, :].rearrange("p i (j e) -> p i j e", e=2),
                 in0=trig[n][:, wave, :, :].unsqueeze(3).to_broadcast([P, PIECE, PAIRS, 2]),
                 in1=factor[:, t, :, :].unsqueeze(1).to_broadcast([P, PIECE, PAIRS, 2]),
@@ -426,6 +426,7 @@ def tile_causalselfattention_pa_t_kernel(
                     reduce_turns(piece)
                     waves(piece)
                 nc.scalar.activation(out=unused[:], in_=zero[:], func=ACT.Sqrt)
+            if n == 2:
                 for part in range(4):
                     fold(0, part)
             if n >= 3 and n < 3 + 4 * (PIECES - 1):

@@ -48,6 +48,7 @@ def tile_causalselfattention_pa_t_kernel(
     with ExitStack() as ctx:
         const = ctx.enter_context(tc.tile_pool(name="const", bufs=1))
         xpool = ctx.enter_context(tc.tile_pool(name="xpool", bufs=UNITS))
+        one = ctx.enter_context(tc.tile_pool(name="one", bufs=1))
         two = ctx.enter_context(tc.tile_pool(name="two", bufs=2))
         three = ctx.enter_context(tc.tile_pool(name="three", bufs=3))
         ps_x = ctx.enter_context(tc.psum_pool(name="ps_x", bufs=2))
@@ -259,7 +260,7 @@ def tile_causalselfattention_pa_t_kernel(
                         )
 
         def times_sine(i):
-            crossed[i] = two.tile([P, 2, H, SUB * C], F32, name="crossed")
+            crossed[i] = one.tile([P, 2, H, SUB * C], F32, name="crossed")
             for t in range(2):
                 nc.gpsimd.tensor_mul(
                     out=crossed[i][:, t, :, :],
@@ -403,12 +404,11 @@ def tile_causalselfattention_pa_t_kernel(
                 normalise(n - 3)
             if live(n - 1) and n > 1:
                 quantise(n - 1)
-            if live(n) and n > 0:
-                regroup(n, 0)
             if live(n - 2):
                 root(n - 2)
             if live(n) and n > 0:
-                regroup(n, 1)
+                for b in range(SUB // 2):
+                    regroup(n, b)
             if live(n - 1):
                 project(n - 1)
             if live(n - 2):

@@ -263,10 +263,12 @@ def tile_causalselfattention_pa_t_kernel(
             crossed[i] = one.tile([P, 2, H, SUB * C], F32, name="crossed")
             for t in range(2):
                 nc.gpsimd.tensor_mul(
-                    out=crossed[i][:, t, :, :],
-                    in0=normed[i][:, t, :, :, :].rearrange("p h s c -> p h (s c)"),
-                    in1=of_unit(sine, i)[:, t, :, :].rearrange("p s c -> p (s c)")
-                    .unsqueeze(1).to_broadcast([P, H, SUB * C]),
+                    out=crossed[i][:, t, :, :].rearrange("p h (n e) -> p h n e", e=2),
+                    in0=normed[i][:, t, :, :, :].rearrange("p h s (j e) -> p h (s j) e", e=2)[
+                        :, :, :, ::-1
+                    ],
+                    in1=of_unit(sine, i)[:, t, :, :].rearrange("p s (j e) -> p (s j) e", e=2)
+                    .unsqueeze(1).to_broadcast([P, H, SUB * PAIRS, 2]),
                 )
 
         def times_cosine(i):
@@ -280,11 +282,7 @@ def tile_causalselfattention_pa_t_kernel(
 
         def finish_qk(i):
             qk_out = three.tile([P, 2, H, SUB * C], F32)
-            nc.vector.tensor_add(
-                out=qk_out[:].rearrange("p t h (n e) -> p (t h n) e", e=2),
-                in0=straight[i][:].rearrange("p t h (n e) -> p (t h n) e", e=2),
-                in1=crossed[i][:].rearrange("p t h (n e) -> p (t h n) e", e=2)[:, :, ::-1],
-            )
+            nc.vector.tensor_add(out=qk_out[:], in0=straight[i][:], in1=crossed[i][:])
             for t, dest in enumerate((out_0, out_1)):
                 nc.sync.dma_start(
                     out=dest[:, i * UNIT : (i + 1) * UNIT, :].rearrange(
@@ -337,8 +335,8 @@ def tile_causalselfattention_pa_t_kernel(
             out=gain[:].rearrange("p t j e -> p (t j e)"), in_=spread[:, 1, 0 : 2 * C]
         )
         signed = const.tile([P, 2, PAIRS, 2], F32)
-        nc.vector.tensor_copy(out=signed[:, :, :, 0], in_=gain[:, :, :, 0])
-        nc.vector.tensor_scalar_mul(out=signed[:, :, :, 1], in0=gain[:, :, :, 1], scalar1=-1.0)
+        nc.vector.tensor_scalar_mul(out=signed[:, :, :, 0], in0=gain[:, :, :, 1], scalar1=-1.0)
+        nc.vector.tensor_copy(out=signed[:, :, :, 1], in_=gain[:, :, :, 0])
         quantise(0)
 
         turns = {}

@@ -5,12 +5,12 @@ from concourse.masks import make_identity
 
 F32 = mybir.dt.float32
 BF16 = mybir.dt.bfloat16
-I32 = mybir.dt.int32
 U32 = mybir.dt.uint32
 U8 = mybir.dt.uint8
 FP8X4 = mybir.dt.float8_e4m3fn_x4
 ALU = mybir.AluOpType
 ACT = mybir.ActivationFunctionType
+AX = mybir.AxisListType
 
 T, D, H, C = 8192, 512, 4, 32
 E = H * C
@@ -19,14 +19,14 @@ BASE = 10000.0
 PI = 3.141592653589793
 
 P = 128
-SUB = 4
+ROWS = 8
+CHUNK = P * ROWS
+CHUNKS = T // CHUNK
+SUB = ROWS // 2
 UNIT = P * SUB
-UNITS = T // UNIT
-POS = UNITS * SUB
+UNITS = 2 * CHUNKS
 PAIRS = C // 2
 GROUPS = 2 * SUB * H
-PIECE = 16
-PIECES = POS // PIECE
 ROUND = 12582912.0
 
 FLOPS = 2 * T * D * 3 * E
@@ -51,10 +51,10 @@ def tile_causalselfattention_pa_t_kernel(
         one = ctx.enter_context(tc.tile_pool(name="one", bufs=1))
         two = ctx.enter_context(tc.tile_pool(name="two", bufs=2))
         three = ctx.enter_context(tc.tile_pool(name="three", bufs=3))
-        ps_x = ctx.enter_context(tc.psum_pool(name="ps_x", bufs=2))
-        ps_c = ctx.enter_context(tc.psum_pool(name="ps_c", bufs=2))
+        ps_io = ctx.enter_context(tc.psum_pool(name="ps_io", bufs=3))
         ps_v = ctx.enter_context(tc.psum_pool(name="ps_v", bufs=1))
         ps_t = ctx.enter_context(tc.psum_pool(name="ps_t", bufs=3))
+        ps_cos = ctx.enter_context(tc.psum_pool(name="ps_cos", bufs=1))
         ctx.enter_context(tc.manual_schedule())
 
         x_rows = {}
@@ -63,21 +63,37 @@ def tile_causalselfattention_pa_t_kernel(
         codes = {}
         scales = {}
         acc = {}
+        acc_v = {}
         biased = {}
         u = {}
         stats = {}
-        std = {}
         rstd = {}
         shift = {}
         normed = {}
         straight = {}
         crossed = {}
+        cosine = {}
+        sine = {}
+
+        def rows_of(i):
+            return slice(SUB * (i % 2), SUB * (i % 2) + SUB)
+
+        def tokens_of(i):
+            return slice((i // 2) * CHUNK, (i // 2 + 1) * CHUNK)
 
         def load(i):
             x_rows[i] = xpool.tile([P, SUB, D], BF16, name="x_rows")
             nc.sync.dma_start(
                 out=x_rows[i][:],
-                in_=x[i * UNIT : (i + 1) * UNIT, :].rearrange("(p s) k -> p s k", s=SUB),
+                in_=x[tokens_of(i), :].rearrange("(p r) k -> p r k", r=ROWS)[:, rows_of(i), :],
+            )
+
+        def store(dest, i, tile):
+            nc.sync.dma_start(
+                out=dest[:, tokens_of(i), :].rearrange("h (p r) c -> p h r c", r=ROWS)[
+                    :, :, rows_of(i), :
+                ],
+                in_=tile,
             )
 
         load(0)
@@ -94,47 +110,125 @@ def tile_causalselfattention_pa_t_kernel(
         nc.scalar.dma_start(
             out=vectors[0:1, 3 * E + C : 3 * E + 2 * C], in_=k_ln_w.rearrange("(o n) -> o n", o=1)
         )
-        ones = const.tile([P, P], BF16)
-        nc.vector.memset(ones[:], 1.0)
-        eps = const.tile([P, 1], F32)
-        nc.vector.memset(eps[:], EPS)
         zero = const.tile([P, 1], F32)
         nc.vector.memset(zero[:], 0.0)
         unused = const.tile([P, 1], F32)
         nc.scalar.activation(out=unused[:], in_=zero[:], func=ACT.Sin)
+        ones = const.tile([P, P], BF16)
+        nc.vector.memset(ones[:], 1.0)
+        eps = const.tile([P, 1], F32)
+        nc.vector.memset(eps[:], EPS)
         ident = const.tile([P, P], F32)
         make_identity(nc, ident[:])
-        pos_i = const.tile([P, POS], I32)
-        nc.gpsimd.iota(pos_i[:], pattern=[[UNIT, UNITS], [1, SUB]], base=0, channel_multiplier=SUB)
 
-        pos = const.tile([P, POS], F32)
-        nc.vector.tensor_copy(out=pos[:], in_=pos_i[:])
-        whole = const.tile([P, PAIRS, POS], F32)
+        lane = const.tile([P, 1], F32)
+        nc.gpsimd.iota(
+            lane[:], pattern=[[1, 1]], base=0, channel_multiplier=1,
+            allow_small_or_imprecise_dtypes=True,
+        )
+        slot = const.tile([P, ROWS, PAIRS], F32)
+        nc.gpsimd.iota(
+            slot[:], pattern=[[PAIRS, ROWS], [1, PAIRS]], base=0, channel_multiplier=0,
+            allow_small_or_imprecise_dtypes=True,
+        )
+        slot_row = const.tile([P, ROWS, PAIRS], F32)
+        nc.gpsimd.iota(
+            slot_row[:], pattern=[[1, ROWS], [0, PAIRS]], base=0, channel_multiplier=0,
+            allow_small_or_imprecise_dtypes=True,
+        )
+        first = const.tile([P, P], F32)
+        nc.gpsimd.iota(
+            first[:], pattern=[[ROWS, P]], base=0, channel_multiplier=0,
+            allow_small_or_imprecise_dtypes=True,
+        )
+        token = const.tile([P, P + CHUNKS], F32)
+        nc.gpsimd.iota(
+            token[:, P:], pattern=[[CHUNK, CHUNKS]], base=0, channel_multiplier=0,
+            allow_small_or_imprecise_dtypes=True,
+        )
+        hot = const.tile([P, ROWS, PAIRS], F32)
+        nc.vector.tensor_scalar(
+            out=hot[:], in0=slot[:], scalar1=lane[:, 0:1], scalar2=None, op0=ALU.is_equal
+        )
+        hot_pair = const.tile([P, PAIRS], F32)
+        nc.vector.reduce_sum(
+            out=hot_pair[:], in_=hot[:].rearrange("p r j -> p j r"), axis=AX.X
+        )
+        own_row = const.tile([P, ROWS, PAIRS], F32)
+        nc.vector.tensor_mul(out=own_row[:], in0=hot[:], in1=slot_row[:])
+        terms = const.tile([P, 2, PAIRS], F32)
         for j in range(PAIRS):
             high, low = split_frequency(j)
+            nc.vector.tensor_scalar_mul(
+                out=terms[:, 0, j : j + 1], in0=hot_pair[:, j : j + 1], scalar1=high
+            )
+            nc.scalar.mul(terms[:, 1, j : j + 1], hot_pair[:, j : j + 1], low)
+        row = const.tile([P, 1], F32)
+        nc.vector.reduce_sum(
+            out=row[:], in_=own_row[:].rearrange("p r j -> p (r j)"), axis=AX.X
+        )
+        frequency = const.tile([P, 2], F32)
+        nc.vector.reduce_sum(out=frequency[:], in_=terms[:], axis=AX.X)
+
+        def fraction(out, turns, scratch):
             nc.vector.tensor_scalar(
-                out=whole[:, j, :], in0=pos[:], scalar1=high, scalar2=ROUND,
-                op0=ALU.mult, op1=ALU.add,
+                out=scratch, in0=turns, scalar1=ROUND, scalar2=ROUND,
+                op0=ALU.add, op1=ALU.subtract,
             )
+            nc.vector.tensor_sub(out=out, in0=turns, in1=scratch)
+
+        nc.vector.tensor_scalar(
+            out=token[:, 0:P], in0=first[:], scalar1=row[:, 0:1], scalar2=None, op0=ALU.add
+        )
+        whole = const.tile([P, P + CHUNKS], F32)
+        nc.vector.tensor_scalar(
+            out=whole[:], in0=token[:], scalar1=frequency[:, 0:1], scalar2=ROUND,
+            op0=ALU.mult, op1=ALU.add,
+        )
         nc.vector.tensor_scalar_sub(out=whole[:], in0=whole[:], scalar1=ROUND)
-        angle = const.tile([P, PAIRS, POS], F32)
-        for j in range(PAIRS):
-            high, low = split_frequency(j)
-            nc.vector.scalar_tensor_tensor(
-                out=whole[:, j, :], in0=pos[:], scalar=high, in1=whole[:, j, :],
-                op0=ALU.mult, op1=ALU.subtract,
+        nc.vector.scalar_tensor_tensor(
+            out=whole[:], in0=token[:], scalar=frequency[:, 0:1], in1=whole[:],
+            op0=ALU.mult, op1=ALU.subtract,
+        )
+        nc.vector.scalar_tensor_tensor(
+            out=whole[:], in0=token[:], scalar=frequency[:, 1:2], in1=whole[:],
+            op0=ALU.mult, op1=ALU.add,
+        )
+        base_turns = const.tile([P, P + CHUNKS], F32)
+        base_scratch = const.tile([P, P + CHUNKS], F32)
+        fraction(base_turns[:], whole[:], base_scratch[:])
+        turns = const.tile([P, CHUNKS, P], F32)
+        turns_scratch = const.tile([P, CHUNKS, P], F32)
+        quarter = const.tile([P, CHUNKS, P], F32)
+        trig = const.tile([P, 2, CHUNKS, P], F32)
+
+        def chunk_turns():
+            nc.vector.tensor_add(
+                out=turns[:],
+                in0=base_turns[:, 0:P].unsqueeze(1).to_broadcast([P, CHUNKS, P]),
+                in1=base_turns[:, P:].unsqueeze(2).to_broadcast([P, CHUNKS, P]),
             )
-        for j in range(PAIRS):
-            high, low = split_frequency(j)
-            nc.vector.scalar_tensor_tensor(
-                out=angle[:, j, :], in0=pos[:], scalar=low, in1=whole[:, j, :],
+            fraction(turns[:], turns[:], turns_scratch[:])
+
+        def sines():
+            nc.scalar.activation(out=quarter[:], in_=turns[:], func=ACT.Abs)
+            nc.scalar.activation(
+                out=trig[:, 0, :, :], in_=turns[:], func=ACT.Sin, scale=2.0 * PI
+            )
+
+        def cosines():
+            nc.vector.tensor_scalar(
+                out=quarter[:], in0=quarter[:], scalar1=-1.0, scalar2=0.25,
                 op0=ALU.mult, op1=ALU.add,
+            )
+            nc.scalar.activation(
+                out=trig[:, 1, :, :], in_=quarter[:], func=ACT.Sin, scale=2.0 * PI
             )
 
         def turn(i):
             x_turned[i] = []
             for b in range(SUB // 2):
-                xt = ps_x.tile([P, 2, 2, P], F32, tag="xt")
+                xt = ps_io.tile([P, 2, 2, P], F32, tag="io")
                 for s in range(2):
                     for half in range(2):
                         nc.tensor.transpose(
@@ -143,14 +237,15 @@ def tile_causalselfattention_pa_t_kernel(
                             ident[:],
                         )
                 x_turned[i].append(xt)
-            grouped[i] = two.tile([P, UNIT * 4], BF16, align_bytes=64, name="grouped")
 
-        def regroup(i, b):
+        def regroup(i):
+            grouped[i] = two.tile([P, UNIT * 4], BF16, align_bytes=64, name="grouped")
             words = grouped[i][:].bitcast(F32).rearrange("p (s m e) -> p s m e", s=SUB, e=2)
-            nc.scalar.copy(
-                out=words[:, 2 * b : 2 * b + 2, :, :],
-                in_=x_turned[i][b][:].rearrange("p s e m -> p s m e"),
-            )
+            for b in range(SUB // 2):
+                nc.scalar.copy(
+                    out=words[:, 2 * b : 2 * b + 2, :, :],
+                    in_=x_turned[i][b][:].rearrange("p s e m -> p s m e"),
+                )
 
         def quantise(i):
             codes[i] = two.tile([P, UNIT], U32, align_bytes=64, name="codes")
@@ -159,10 +254,10 @@ def tile_causalselfattention_pa_t_kernel(
                 out=codes[i][:].bitcast(FP8X4), scales=scales[i][:], in_=grouped[i][:]
             )
 
-        def project(i):
+        def project_qk(i):
             acc[i] = []
             for t in range(2):
-                cm = ps_c.tile([P, UNIT], F32, tag="cm")
+                cm = ps_io.tile([P, UNIT], F32, tag="io")
                 nc.tensor.matmul_mx(
                     out=cm[:],
                     lhsT=w_codes[:, t * E : (t + 1) * E].bitcast(FP8X4),
@@ -171,17 +266,18 @@ def tile_causalselfattention_pa_t_kernel(
                     start=True, stop=True,
                 )
                 acc[i].append(cm)
-            av = ps_v.tile([P, SUB, E], F32, tag="av")
+
+        def project_v(i):
+            acc_v[i] = ps_v.tile([P, SUB, E], F32, tag="av", name="acc_v")
             for s in range(SUB):
                 cols = slice(s * P, (s + 1) * P)
                 nc.tensor.matmul_mx(
-                    out=av[:, s, :],
+                    out=acc_v[i][:, s, :],
                     lhsT=codes[i][:, cols].bitcast(FP8X4), lhsT_scale=scales[i][:, cols],
                     rhs=w_codes[:, 2 * E : 3 * E].bitcast(FP8X4),
                     rhs_scale=w_scales[:, 2 * E : 3 * E],
                     start=True, stop=True,
                 )
-            acc[i].append(av)
 
         def add_bias(i):
             biased[i] = []
@@ -192,53 +288,41 @@ def tile_causalselfattention_pa_t_kernel(
                 )
                 biased[i].append(cb)
 
-        def turn_back(i):
-            u[i] = []
-            for t in range(2):
-                tm = ps_t.tile([P, SUB, E], F32, tag="tm")
-                for s in range(SUB):
-                    nc.tensor.transpose(
-                        tm[:, s, :], biased[i][t][:, s * P : (s + 1) * P], ident[:]
-                    )
-                u[i].append(tm)
+        def turn_back(i, t):
+            tm = ps_t.tile([P, SUB, E], F32, tag="tm")
+            for s in range(SUB):
+                nc.tensor.transpose(tm[:, s, :], biased[i][t][:, s * P : (s + 1) * P], ident[:])
+            u[i, t] = tm
 
         def finish_v(i):
             v_out = three.tile([P, H, SUB, C], F32)
             nc.vector.tensor_add(
                 out=v_out[:],
-                in0=acc[i][2][:].rearrange("p s (h c) -> p h s c", c=C),
+                in0=acc_v[i][:].rearrange("p s (h c) -> p h s c", c=C),
                 in1=bias_v[:].rearrange("p (h c) -> p h c", c=C).unsqueeze(2)
                 .to_broadcast([P, H, SUB, C]),
             )
-            nc.sync.dma_start(
-                out=out_2[:, i * UNIT : (i + 1) * UNIT, :].rearrange(
-                    "h (p s) c -> p h (s c)", s=SUB
-                ),
-                in_=v_out[:].rearrange("p h s c -> p h (s c)"),
-            )
+            store(out_2, i, v_out[:])
 
-        def measure(i):
-            stats[i] = three.tile([P, GROUPS, 3], F32, name="stats")
-            for t in range(2):
-                for s in range(SUB):
-                    for h in range(0, H, 2):
-                        g = (t * SUB + s) * H + h
-                        nc.vector.bn_stats(
-                            out=stats[i][:, g : g + 2, :].rearrange("p two k -> p (two k)"),
-                            in_=u[i][t][:, s, h * C : (h + 2) * C].rearrange(
-                                "p (two c) -> p c two", two=2
-                            ),
-                        )
-
-        def root(i):
-            std[i] = three.tile([P, GROUPS], F32, name="std")
-            nc.scalar.activation(
-                out=std[i][:], in_=stats[i][:, :, 2], func=ACT.Sqrt, scale=1.0 / C, bias=eps[:]
-            )
+        def measure(i, t):
+            if t == 0:
+                stats[i] = three.tile([P, GROUPS, 3], F32, name="stats")
+            for s in range(SUB):
+                for h in range(0, H, 2):
+                    g = (t * SUB + s) * H + h
+                    nc.vector.bn_stats(
+                        out=stats[i][:, g : g + 2, :].rearrange("p two k -> p (two k)"),
+                        in_=u[i, t][:, s, h * C : (h + 2) * C].rearrange(
+                            "p (two c) -> p c two", two=2
+                        ),
+                    )
 
         def invert(i):
             rstd[i] = three.tile([P, GROUPS], F32, name="rstd")
-            nc.vector.reciprocal(out=rstd[i][:], in_=std[i][:])
+            nc.scalar.activation(
+                out=rstd[i][:], in_=stats[i][:, :, 2], func=ACT.Abs_reciprocal_sqrt,
+                scale=1.0 / C, bias=eps[:],
+            )
 
         def offset(i):
             shift[i] = three.tile([P, GROUPS], F32, name="shift")
@@ -247,51 +331,68 @@ def tile_causalselfattention_pa_t_kernel(
                 op0=ALU.mult, op1=ALU.mult,
             )
 
-        def normalise(i):
-            normed[i] = three.tile([P, 2, H, SUB, C], F32, name="normed")
-            for t in range(2):
-                for s in range(SUB):
-                    for h in range(H):
-                        g = (t * SUB + s) * H + h
-                        nc.scalar.activation(
-                            out=normed[i][:, t, h, s, :],
-                            in_=u[i][t][:, s, h * C : (h + 1) * C], func=ACT.Identity,
-                            scale=rstd[i][:, g : g + 1], bias=shift[i][:, g : g + 1],
-                        )
+        def normalise(i, t):
+            if t == 0:
+                normed[i] = three.tile([P, 2, H, SUB, C], F32, name="normed")
+            for s in range(SUB):
+                for h in range(H):
+                    g = (t * SUB + s) * H + h
+                    nc.scalar.activation(
+                        out=normed[i][:, t, h, s, :],
+                        in_=u[i, t][:, s, h * C : (h + 1) * C], func=ACT.Identity,
+                        scale=rstd[i][:, g : g + 1], bias=shift[i][:, g : g + 1],
+                    )
 
-        def times_sine(i):
-            crossed[i] = one.tile([P, 2, H, SUB * C], F32, name="crossed")
-            for t in range(2):
-                nc.gpsimd.tensor_mul(
-                    out=crossed[i][:, t, :, :].rearrange("p h (n e) -> p h n e", e=2),
-                    in0=normed[i][:, t, :, :, :].rearrange("p h s (j e) -> p h (s j) e", e=2)[
-                        :, :, :, ::-1
-                    ],
-                    in1=of_unit(sine, i)[:, t, :, :].rearrange("p s (j e) -> p (s j) e", e=2)
-                    .unsqueeze(1).to_broadcast([P, H, SUB * PAIRS, 2]),
-                )
-
-        def times_cosine(i):
-            straight[i] = two.tile([P, 2, H, SUB * C], F32, name="straight")
-            nc.vector.tensor_mul(
-                out=straight[i][:],
-                in0=normed[i][:].rearrange("p t h s c -> p t h (s c)"),
-                in1=of_unit(cosine, i).rearrange("p t s c -> p t (s c)")
-                .unsqueeze(2).to_broadcast([P, 2, H, SUB * C]),
+        def times_sine(i, t, engine):
+            if t == 0:
+                crossed[i] = one.tile([P, 2, H, SUB, C], F32, name="crossed")
+            engine.tensor_mul(
+                out=crossed[i][:, t, :, :, :].rearrange("p h s (j e) -> p h (s j) e", e=2),
+                in0=normed[i][:, t, :, :, :].rearrange("p h s (j e) -> p h (s j) e", e=2)[
+                    :, :, :, ::-1
+                ],
+                in1=sine[i // 2][:, t, rows_of(i), :].rearrange("p s (j e) -> p (s j) e", e=2)
+                .unsqueeze(1).to_broadcast([P, H, SUB * PAIRS, 2]),
             )
 
-        def finish_qk(i):
-            qk_out = three.tile([P, 2, H, SUB * C], F32)
-            nc.vector.tensor_add(out=qk_out[:], in0=straight[i][:], in1=crossed[i][:])
-            for t, dest in enumerate((out_0, out_1)):
-                nc.sync.dma_start(
-                    out=dest[:, i * UNIT : (i + 1) * UNIT, :].rearrange(
-                        "h (p s) c -> p h (s c)", s=SUB
-                    ),
-                    in_=qk_out[:, t, :, :],
-                )
+        def times_cosine(i, ts):
+            if ts.start == 0:
+                straight[i] = two.tile([P, 2, H, SUB, C], F32, name="straight")
+            n = ts.stop - ts.start
+            nc.vector.tensor_mul(
+                out=straight[i][:, ts, :, :, :].rearrange("p t h s c -> p t h (s c)"),
+                in0=normed[i][:, ts, :, :, :].rearrange("p t h s c -> p t h (s c)"),
+                in1=cosine[i // 2][:, ts, rows_of(i), :].rearrange("p t s c -> p t (s c)")
+                .unsqueeze(2).to_broadcast([P, n, H, SUB * C]),
+            )
+
+        def finish_qk(i, ts):
+            qk_out = three.tile([P, 2, H, SUB, C], F32)
+            nc.vector.tensor_add(
+                out=qk_out[:, ts, :, :, :], in0=straight[i][:, ts, :, :, :],
+                in1=crossed[i][:, ts, :, :, :],
+            )
+            for t in range(ts.start, ts.stop):
+                store((out_0, out_1)[t], i, qk_out[:, t, :, :, :])
+
+        def sine_table(b):
+            product = ps_io.tile([P, 2, ROWS, C], F32, tag="io")
+            nc.tensor.matmul(
+                out=product[:].rearrange("p t r c -> p (t r c)"), lhsT=trig[:, 0, b, :],
+                rhs=mix_sine[:].rearrange("p t r j e -> p (t r j e)"), start=True, stop=True,
+            )
+            sine[b] = two.tile([P, 2, ROWS, C], F32, name="sine")
+            nc.scalar.copy(out=sine[b][:], in_=product[:])
+
+        def cosine_table(b):
+            cosine[b] = ps_cos.tile([P, 2, ROWS, C], F32, tag="cosine", name="cosine")
+            nc.tensor.matmul(
+                out=cosine[b][:].rearrange("p t r c -> p (t r c)"), lhsT=trig[:, 1, b, :],
+                rhs=mix_cosine[:].rearrange("p t r j e -> p (t r j e)"), start=True, stop=True,
+            )
 
         turn(0)
+        regroup(0)
         w_grouped = const.tile([P, 3 * E * 4], BF16, align_bytes=64)
         w_words = w_grouped[:].bitcast(F32).rearrange("p (a r e) -> p a r e", a=3, e=2)
         w_codes = const.tile([P, 3 * E], U32, align_bytes=64)
@@ -302,20 +403,18 @@ def tile_causalselfattention_pa_t_kernel(
                 nc.tensor.transpose(
                     wt[:, half, :], w_rows[:, a, :].bitcast(F32)[:, half : 2 * P : 2], ident[:]
                 )
-            nc.vector.tensor_copy(
+            nc.scalar.copy(
                 out=w_words[:, a, :, :], in_=wt[:, 0:2, :].rearrange("p e r -> p r e")
             )
-        for b in range(SUB // 2):
-            regroup(0, b)
         nc.vector.quantize_mx(
             out=w_codes[:, 0 : 2 * E].bitcast(FP8X4), scales=w_scales[:, 0 : 2 * E],
             in_=w_grouped[:, 0 : 2 * E * 4],
         )
+        quantise(0)
         nc.vector.quantize_mx(
             out=w_codes[:, 2 * E : 3 * E].bitcast(FP8X4), scales=w_scales[:, 2 * E : 3 * E],
             in_=w_grouped[:, 2 * E * 4 : 3 * E * 4],
         )
-
         spread = ps_v.tile([P, SUB, E], F32, tag="av")
         nc.tensor.matmul(
             out=spread[:, 0:2, :].rearrange("p s c -> p (s c)"), lhsT=ones[:],
@@ -323,11 +422,11 @@ def tile_causalselfattention_pa_t_kernel(
         )
         for t in range(2):
             nc.tensor.matmul(
-                out=spread[:, 2 + t, :], lhsT=vectors[:, t * E : (t + 1) * E], rhs=ones[:],
-                start=True, stop=True,
+                out=spread[:, 2, 4 * t : 4 * t + 4], lhsT=vectors[:, t * E : (t + 1) * E],
+                rhs=ones[:, 0:4], start=True, stop=True,
             )
         bias_qk = const.tile([P, 2], F32)
-        nc.vector.tensor_copy(out=bias_qk[:], in_=spread[:, 2:4, 0])
+        nc.vector.tensor_copy(out=bias_qk[:], in_=spread[:, 2, 0:8:4])
         bias_v = const.tile([P, E], F32)
         nc.vector.tensor_copy(out=bias_v[:], in_=spread[:, 0, :])
         gain = const.tile([P, 2, PAIRS, 2], F32)
@@ -337,95 +436,76 @@ def tile_causalselfattention_pa_t_kernel(
         signed = const.tile([P, 2, PAIRS, 2], F32)
         nc.vector.tensor_scalar_mul(out=signed[:, :, :, 0], in0=gain[:, :, :, 1], scalar1=-1.0)
         nc.vector.tensor_copy(out=signed[:, :, :, 1], in_=gain[:, :, :, 0])
-        quantise(0)
+        mix_cosine = const.tile([P, 2, ROWS, PAIRS, 2], F32)
+        mix_sine = const.tile([P, 2, ROWS, PAIRS, 2], F32)
+        for mix, factor in ((mix_sine, signed), (mix_cosine, gain)):
+            for t in range(2):
+                nc.gpsimd.tensor_mul(
+                    out=mix[:, t, :, :, :],
+                    in0=hot[:].unsqueeze(3).to_broadcast([P, ROWS, PAIRS, 2]),
+                    in1=factor[:, t, :, :].unsqueeze(1).to_broadcast([P, ROWS, PAIRS, 2]),
+                )
 
-        turns = {}
-        trig = {}
-        cosine = {}
-        sine = {}
-
-        def reduce_turns(n):
-            here = angle[:, :, n * PIECE : (n + 1) * PIECE]
-            turns[n] = const.tile([P, 2, PAIRS, PIECE], F32, name="turns" + str(n))
-            nearest = const.tile([P, 2, PAIRS, PIECE], F32, name="nearest" + str(n))
-            nc.vector.tensor_scalar_add(out=turns[n][:, 1, :, :], in0=here, scalar1=0.25)
-            nc.vector.tensor_scalar(
-                out=nearest[:, 0, :, :], in0=here, scalar1=ROUND, scalar2=ROUND,
-                op0=ALU.add, op1=ALU.subtract,
-            )
-            nc.vector.tensor_scalar(
-                out=nearest[:, 1, :, :], in0=turns[n][:, 1, :, :], scalar1=ROUND, scalar2=ROUND,
-                op0=ALU.add, op1=ALU.subtract,
-            )
-            nc.vector.tensor_sub(out=turns[n][:, 0, :, :], in0=here, in1=nearest[:, 0, :, :])
-            nc.vector.tensor_sub(
-                out=turns[n][:, 1, :, :], in0=turns[n][:, 1, :, :], in1=nearest[:, 1, :, :]
-            )
-
-        def waves(n):
-            trig[n] = const.tile([P, 2, PIECE, PAIRS], F32, name="trig" + str(n))
-            nc.scalar.activation(
-                out=trig[n][:], in_=turns[n][:].rearrange("p w j i -> p w i j"),
-                func=ACT.Sin, scale=2.0 * PI,
-            )
-
-        def fold(n, part):
-            t = part % 2
-            if part == 0:
-                cosine[n] = const.tile([P, 2, PIECE, C], F32, name="cosine" + str(n))
-                sine[n] = const.tile([P, 2, PIECE, C], F32, name="sine" + str(n))
-            table, wave, factor = ((cosine, 1, gain), (sine, 0, signed))[part // 2]
-            nc.vector.tensor_mul(
-                out=table[n][:, t, :, :].rearrange("p i (j e) -> p i j e", e=2),
-                in0=trig[n][:, wave, :, :].unsqueeze(3).to_broadcast([P, PIECE, PAIRS, 2]),
-                in1=factor[:, t, :, :].unsqueeze(1).to_broadcast([P, PIECE, PAIRS, 2]),
-            )
-
-        def of_unit(table, i):
-            first = i * SUB % PIECE
-            return table[i * SUB // PIECE][:, :, first : first + SUB, :]
+        chunk_turns()
 
         def live(i):
             return 0 <= i < UNITS
 
-        for n in range(UNITS + 4):
+        both = slice(0, 2)
+        LAST = UNITS - 1
+        for n in range(1, UNITS + 3):
+            roped = live(n - 4) and n - 4 < LAST - 1
+            if roped:
+                for t in range(2):
+                    times_sine(n - 4, t, nc.gpsimd)
             if live(n - 2):
-                turn_back(n - 2)
-            if live(n - 4):
-                times_sine(n - 4)
-            if live(n) and n > 0:
-                turn(n)
-            if live(n - 2):
-                finish_v(n - 2)
-                measure(n - 2)
-            if live(n - 3):
-                normalise(n - 3)
+                turn_back(n - 2, 0)
             if live(n - 1) and n > 1:
                 quantise(n - 1)
-            if live(n - 2):
-                root(n - 2)
-            if live(n) and n > 0:
-                for b in range(SUB // 2):
-                    regroup(n, b)
-            if live(n - 1):
-                project(n - 1)
-            if live(n - 2):
-                invert(n - 2)
             if live(n - 3):
-                times_cosine(n - 3)
+                normalise(n - 3, 0)
+            if live(n - 1):
+                project_qk(n - 1)
             if live(n - 2):
-                offset(n - 2)
-            if live(n - 4):
-                finish_qk(n - 4)
+                measure(n - 2, 0)
+            if n == 2:
+                cosines()
+                nc.scalar.activation(out=unused[:], in_=eps[:], func=ACT.Abs_reciprocal_sqrt)
+            if live(n - 2):
+                turn_back(n - 2, 1)
+                finish_v(n - 2)
+            if live(n - 1):
+                project_v(n - 1)
+            if live(n - 2):
+                measure(n - 2, 1)
             if live(n - 1):
                 add_bias(n - 1)
+            if live(n - 2):
+                invert(n - 2)
+            if live(n):
+                turn(n)
+            if roped:
+                times_cosine(n - 4, both)
+            if live(n - 3):
+                normalise(n - 3, 1)
+            if roped:
+                finish_qk(n - 4, both)
+            if live(n - 2):
+                offset(n - 2)
+            if live(n):
+                regroup(n)
             if n == 1:
-                for piece in range(PIECES):
-                    reduce_turns(piece)
-                    waves(piece)
-                nc.scalar.activation(out=unused[:], in_=zero[:], func=ACT.Sqrt)
-            if n == 2:
-                for part in range(4):
-                    fold(0, part)
-            if n >= 3 and n < 3 + 4 * (PIECES - 1):
-                fold((n + 1) // 4, (n + 1) % 4)
+                sines()
+            if n % 2 == 0 and n // 2 - 1 < CHUNKS:
+                sine_table(n // 2 - 1)
+            if n % 2 == 1 and n >= 3 and (n - 3) // 2 < CHUNKS:
+                cosine_table((n - 3) // 2)
+            if n > LAST:
+                last = n - 3
+                if last >= LAST - 1:
+                    for t in range(2):
+                        times_cosine(last, slice(t, t + 1))
+                    times_sine(last, 0, nc.gpsimd)
+                    times_sine(last, 1, nc.vector)
+                    for t in range(2):
+                        finish_qk(last, slice(t, t + 1))

@@ -73,6 +73,7 @@ def tile_causalselfattention_pa_t_kernel(
         straight = {}
         crossed = {}
         cosine = {}
+        sine_raw = {}
         sine = {}
 
         def rows_of(i):
@@ -99,17 +100,17 @@ def tile_causalselfattention_pa_t_kernel(
         load(0)
         w_rows = const.tile([P, 3, D], BF16)
         nc.sync.dma_start(out=w_rows[:], in_=W_attn.rearrange("(a p) k -> p a k", p=P))
-        for i in range(1, UNITS):
-            load(i)
         vectors = const.tile([P, 4 * E], BF16)
         nc.vector.memset(vectors[:], 0.0)
-        nc.scalar.dma_start(out=vectors[0:1, 0 : 3 * E], in_=b_attn.rearrange("(o n) -> o n", o=1))
-        nc.scalar.dma_start(
+        nc.sync.dma_start(out=vectors[0:1, 0 : 3 * E], in_=b_attn.rearrange("(o n) -> o n", o=1))
+        nc.sync.dma_start(
             out=vectors[0:1, 3 * E : 3 * E + C], in_=q_ln_w.rearrange("(o n) -> o n", o=1)
         )
-        nc.scalar.dma_start(
+        nc.sync.dma_start(
             out=vectors[0:1, 3 * E + C : 3 * E + 2 * C], in_=k_ln_w.rearrange("(o n) -> o n", o=1)
         )
+        for i in range(1, UNITS):
+            load(i)
         zero = const.tile([P, 1], F32)
         nc.vector.memset(zero[:], 0.0)
         unused = const.tile([P, 1], F32)
@@ -118,8 +119,9 @@ def tile_causalselfattention_pa_t_kernel(
         nc.vector.memset(ones[:], 1.0)
         eps = const.tile([P, 1], F32)
         nc.vector.memset(eps[:], EPS)
-        ident = const.tile([P, P], F32)
-        make_identity(nc, ident[:])
+        highs = const.tile([P, PAIRS], F32)
+        for j in range(PAIRS):
+            nc.vector.memset(highs[:, j : j + 1], split_frequency(j)[0])
 
         lane = const.tile([P, 1], F32)
         nc.gpsimd.iota(
@@ -146,6 +148,8 @@ def tile_causalselfattention_pa_t_kernel(
             token[:, P:], pattern=[[CHUNK, CHUNKS]], base=0, channel_multiplier=0,
             allow_small_or_imprecise_dtypes=True,
         )
+        ident = const.tile([P, P], F32)
+        make_identity(nc, ident[:])
         hot = const.tile([P, ROWS, PAIRS], F32)
         nc.vector.tensor_scalar(
             out=hot[:], in0=slot[:], scalar1=lane[:, 0:1], scalar2=None, op0=ALU.is_equal
@@ -156,19 +160,17 @@ def tile_causalselfattention_pa_t_kernel(
         )
         own_row = const.tile([P, ROWS, PAIRS], F32)
         nc.vector.tensor_mul(out=own_row[:], in0=hot[:], in1=slot_row[:])
-        terms = const.tile([P, 2, PAIRS], F32)
+        high_terms = const.tile([P, PAIRS], F32)
+        nc.vector.tensor_mul(out=high_terms[:], in0=hot_pair[:], in1=highs[:])
+        low_terms = const.tile([P, PAIRS], F32)
         for j in range(PAIRS):
-            high, low = split_frequency(j)
-            nc.vector.tensor_scalar_mul(
-                out=terms[:, 0, j : j + 1], in0=hot_pair[:, j : j + 1], scalar1=high
-            )
-            nc.scalar.mul(terms[:, 1, j : j + 1], hot_pair[:, j : j + 1], low)
+            nc.scalar.mul(low_terms[:, j : j + 1], hot_pair[:, j : j + 1], split_frequency(j)[1])
         row = const.tile([P, 1], F32)
         nc.vector.reduce_sum(
             out=row[:], in_=own_row[:].rearrange("p r j -> p (r j)"), axis=AX.X
         )
         frequency = const.tile([P, 2], F32)
-        nc.vector.reduce_sum(out=frequency[:], in_=terms[:], axis=AX.X)
+        nc.vector.reduce_sum(out=frequency[:, 0:1], in_=high_terms[:], axis=AX.X)
 
         def fraction(out, turns, scratch):
             nc.vector.tensor_scalar(
@@ -190,6 +192,7 @@ def tile_causalselfattention_pa_t_kernel(
             out=whole[:], in0=token[:], scalar=frequency[:, 0:1], in1=whole[:],
             op0=ALU.mult, op1=ALU.subtract,
         )
+        nc.vector.reduce_sum(out=frequency[:, 1:2], in_=low_terms[:], axis=AX.X)
         nc.vector.scalar_tensor_tensor(
             out=whole[:], in0=token[:], scalar=frequency[:, 1:2], in1=whole[:],
             op0=ALU.mult, op1=ALU.add,
@@ -197,55 +200,56 @@ def tile_causalselfattention_pa_t_kernel(
         base_turns = const.tile([P, P + CHUNKS], F32)
         base_scratch = const.tile([P, P + CHUNKS], F32)
         fraction(base_turns[:], whole[:], base_scratch[:])
-        turns = const.tile([P, CHUNKS, P], F32)
-        turns_scratch = const.tile([P, CHUNKS, P], F32)
-        quarter = const.tile([P, CHUNKS, P], F32)
-        trig = const.tile([P, 2, CHUNKS, P], F32)
+        quarter = const.tile([P, P + CHUNKS], F32)
+        base = const.tile([P, 2, P + CHUNKS], F32)
+        minus_sine = const.tile([P, CHUNKS], F32)
+        trig = {0: base}
 
-        def chunk_turns():
-            nc.vector.tensor_add(
-                out=turns[:],
-                in0=base_turns[:, 0:P].unsqueeze(1).to_broadcast([P, CHUNKS, P]),
-                in1=base_turns[:, P:].unsqueeze(2).to_broadcast([P, CHUNKS, P]),
-            )
-            fraction(turns[:], turns[:], turns_scratch[:])
-
-        def sines():
-            nc.scalar.activation(out=quarter[:], in_=turns[:], func=ACT.Abs)
+        def base_sines():
+            nc.scalar.activation(out=quarter[:], in_=base_turns[:], func=ACT.Abs)
             nc.scalar.activation(
-                out=trig[:, 0, :, :], in_=turns[:], func=ACT.Sin, scale=2.0 * PI
+                out=base[:, 0, :], in_=base_turns[:], func=ACT.Sin, scale=2.0 * PI
             )
-
-        def cosines():
             nc.vector.tensor_scalar(
                 out=quarter[:], in0=quarter[:], scalar1=-1.0, scalar2=0.25,
                 op0=ALU.mult, op1=ALU.add,
             )
+
+        def base_cosines():
+            nc.scalar.activation(out=base[:, 1, :], in_=quarter[:], func=ACT.Sin, scale=2.0 * PI)
+
+        def turn_waves(b):
+            scaled = two.tile([P, 2, P], F32)
             nc.scalar.activation(
-                out=trig[:, 1, :, :], in_=quarter[:], func=ACT.Sin, scale=2.0 * PI
+                out=scaled[:], in_=base[:, :, 0:P], func=ACT.Copy,
+                scale=base[:, 1, P + b : P + b + 1],
             )
-
-        def turn(i):
-            x_turned[i] = []
-            for b in range(SUB // 2):
-                xt = ps_io.tile([P, 2, 2, P], F32, tag="io")
-                for s in range(2):
-                    for half in range(2):
-                        nc.tensor.transpose(
-                            xt[:, s, half, :],
-                            x_rows[i][:, 2 * b + s, :].bitcast(F32)[:, half : 2 * P : 2],
-                            ident[:],
-                        )
-                x_turned[i].append(xt)
-
-        def regroup(i):
-            grouped[i] = two.tile([P, UNIT * 4], BF16, align_bytes=64, name="grouped")
-            words = grouped[i][:].bitcast(F32).rearrange("p (s m e) -> p s m e", s=SUB, e=2)
-            for b in range(SUB // 2):
-                nc.scalar.copy(
-                    out=words[:, 2 * b : 2 * b + 2, :, :],
-                    in_=x_turned[i][b][:].rearrange("p s e m -> p s m e"),
+            trig[b] = const.tile([P, 2, P], F32, name="trig" + str(b))
+            for wave, factor in ((0, base[:, 0, P + b : P + b + 1]), (1, minus_sine[:, b : b + 1])):
+                nc.vector.scalar_tensor_tensor(
+                    out=trig[b][:, wave, :], in0=base[:, 1 - wave, 0:P], scalar=factor,
+                    in1=scaled[:, wave, :], op0=ALU.mult, op1=ALU.add,
                 )
+
+        def turn(i, b):
+            xt = ps_io.tile([P, 2, 2, P], F32, tag="io")
+            for s in range(2):
+                for half in range(2):
+                    nc.tensor.transpose(
+                        xt[:, s, half, :],
+                        x_rows[i][:, 2 * b + s, :].bitcast(F32)[:, half : 2 * P : 2],
+                        ident[:],
+                    )
+            x_turned[i, b] = xt
+
+        def regroup(i, b, copy):
+            if b == 0:
+                grouped[i] = two.tile([P, UNIT * 4], BF16, align_bytes=64, name="grouped")
+            words = grouped[i][:].bitcast(F32).rearrange("p (s m e) -> p s m e", s=SUB, e=2)
+            copy(
+                out=words[:, 2 * b : 2 * b + 2, :, :],
+                in_=x_turned[i, b][:].rearrange("p s e m -> p s m e"),
+            )
 
         def quantise(i):
             codes[i] = two.tile([P, UNIT], U32, align_bytes=64, name="codes")
@@ -332,90 +336,102 @@ def tile_causalselfattention_pa_t_kernel(
             )
 
         def normalise(i, t):
-            if t == 0:
-                normed[i] = three.tile([P, 2, H, SUB, C], F32, name="normed")
+            normed[i, t] = two.tile([P, H, SUB, C], F32, name="normed" + str(t))
             for s in range(SUB):
                 for h in range(H):
                     g = (t * SUB + s) * H + h
                     nc.scalar.activation(
-                        out=normed[i][:, t, h, s, :],
+                        out=normed[i, t][:, h, s, :],
                         in_=u[i, t][:, s, h * C : (h + 1) * C], func=ACT.Identity,
                         scale=rstd[i][:, g : g + 1], bias=shift[i][:, g : g + 1],
                     )
 
         def times_sine(i, t, engine):
-            if t == 0:
-                crossed[i] = one.tile([P, 2, H, SUB, C], F32, name="crossed")
+            crossed[i, t] = one.tile([P, H, SUB, C], F32, name="crossed" + str(t))
             engine.tensor_mul(
-                out=crossed[i][:, t, :, :, :].rearrange("p h s (j e) -> p h (s j) e", e=2),
-                in0=normed[i][:, t, :, :, :].rearrange("p h s (j e) -> p h (s j) e", e=2)[
-                    :, :, :, ::-1
-                ],
-                in1=sine[i // 2][:, t, rows_of(i), :].rearrange("p s (j e) -> p (s j) e", e=2)
+                out=crossed[i, t][:].rearrange("p h s (j e) -> p h (s j) e", e=2),
+                in0=normed[i, t][:].rearrange("p h s (j e) -> p h (s j) e", e=2)[:, :, :, ::-1],
+                in1=sine[i][:, t, :, :].rearrange("p s (j e) -> p (s j) e", e=2)
                 .unsqueeze(1).to_broadcast([P, H, SUB * PAIRS, 2]),
             )
 
-        def times_cosine(i, ts):
-            if ts.start == 0:
-                straight[i] = two.tile([P, 2, H, SUB, C], F32, name="straight")
-            n = ts.stop - ts.start
+        def times_cosine(i, t):
+            straight[i, t] = two.tile([P, H, SUB, C], F32, name="straight" + str(t))
             nc.vector.tensor_mul(
-                out=straight[i][:, ts, :, :, :].rearrange("p t h s c -> p t h (s c)"),
-                in0=normed[i][:, ts, :, :, :].rearrange("p t h s c -> p t h (s c)"),
-                in1=cosine[i // 2][:, ts, rows_of(i), :].rearrange("p t s c -> p t (s c)")
-                .unsqueeze(2).to_broadcast([P, n, H, SUB * C]),
+                out=straight[i, t][:].rearrange("p h s c -> p h (s c)"),
+                in0=normed[i, t][:].rearrange("p h s c -> p h (s c)"),
+                in1=cosine[i][:, t, :, :].rearrange("p s c -> p (s c)")
+                .unsqueeze(1).to_broadcast([P, H, SUB * C]),
             )
 
-        def finish_qk(i, ts):
-            qk_out = three.tile([P, 2, H, SUB, C], F32)
-            nc.vector.tensor_add(
-                out=qk_out[:, ts, :, :, :], in0=straight[i][:, ts, :, :, :],
-                in1=crossed[i][:, ts, :, :, :],
-            )
-            for t in range(ts.start, ts.stop):
-                store((out_0, out_1)[t], i, qk_out[:, t, :, :, :])
+        def finish_qk(i, t):
+            qk_out = three.tile([P, H, SUB, C], F32, name="qk_out" + str(t))
+            nc.vector.tensor_add(out=qk_out[:], in0=straight[i, t][:], in1=crossed[i, t][:])
+            store((out_0, out_1)[t], i, qk_out[:])
 
-        def sine_table(b):
-            product = ps_io.tile([P, 2, ROWS, C], F32, tag="io")
+        def gained(out, i, wave):
             nc.tensor.matmul(
-                out=product[:].rearrange("p t r c -> p (t r c)"), lhsT=trig[:, 0, b, :],
-                rhs=mix_sine[:].rearrange("p t r j e -> p (t r j e)"), start=True, stop=True,
-            )
-            sine[b] = two.tile([P, 2, ROWS, C], F32, name="sine")
-            nc.scalar.copy(out=sine[b][:], in_=product[:])
-
-        def cosine_table(b):
-            cosine[b] = ps_cos.tile([P, 2, ROWS, C], F32, tag="cosine", name="cosine")
-            nc.tensor.matmul(
-                out=cosine[b][:].rearrange("p t r c -> p (t r c)"), lhsT=trig[:, 1, b, :],
-                rhs=mix_cosine[:].rearrange("p t r j e -> p (t r j e)"), start=True, stop=True,
+                out=out.rearrange("p t s c -> p (t s c)"), lhsT=trig[i // 2][:, wave, 0:P],
+                rhs=mix[:, wave, i % 2, :, :, :].rearrange("p t s c -> p (t s c)"),
+                start=True, stop=True,
             )
 
-        turn(0)
-        regroup(0)
+        def sine_product(i):
+            sine_raw[i] = ps_io.tile([P, 2, SUB, C], F32, tag="io", name="sine_raw")
+            gained(sine_raw[i][:], i, 0)
+
+        def sine_copy(i):
+            sine[i] = two.tile([P, 2, SUB, C], F32, name="sine")
+            nc.scalar.copy(out=sine[i][:], in_=sine_raw[i][:])
+
+        def cosine_product(i):
+            cosine[i] = ps_cos.tile([P, 2, SUB, C], F32, tag="cosine", name="cosine")
+            gained(cosine[i][:], i, 1)
+
         w_grouped = const.tile([P, 3 * E * 4], BF16, align_bytes=64)
         w_words = w_grouped[:].bitcast(F32).rearrange("p (a r e) -> p a r e", a=3, e=2)
         w_codes = const.tile([P, 3 * E], U32, align_bytes=64)
         w_scales = const.tile([P, 3 * E], U8, align_bytes=64)
-        for a in range(3):
+        w_turned = []
+
+        def quantise_w(a, b):
+            nc.vector.quantize_mx(
+                out=w_codes[:, a * E : b * E].bitcast(FP8X4), scales=w_scales[:, a * E : b * E],
+                in_=w_grouped[:, a * E * 4 : b * E * 4],
+            )
+
+        def turn_w(a):
             wt = ps_t.tile([P, SUB, E], F32, tag="tm")
             for half in range(2):
                 nc.tensor.transpose(
                     wt[:, half, :], w_rows[:, a, :].bitcast(F32)[:, half : 2 * P : 2], ident[:]
                 )
-            nc.scalar.copy(
-                out=w_words[:, a, :, :], in_=wt[:, 0:2, :].rearrange("p e r -> p r e")
+            w_turned.append(wt)
+
+        def regroup_w(a, copy):
+            copy(
+                out=w_words[:, a, :, :],
+                in_=w_turned[a][:, 0:2, :].rearrange("p e r -> p r e"),
             )
-        nc.vector.quantize_mx(
-            out=w_codes[:, 0 : 2 * E].bitcast(FP8X4), scales=w_scales[:, 0 : 2 * E],
-            in_=w_grouped[:, 0 : 2 * E * 4],
-        )
+
+        for b in range(2):
+            turn(0, b)
+        for a in range(3):
+            turn_w(a)
+        turn(1, 0)
+        regroup(0, 0, nc.scalar.copy)
+        regroup(0, 1, nc.vector.tensor_copy)
+        base_sines()
+        regroup_w(0, nc.scalar.copy)
+        regroup_w(1, nc.vector.tensor_copy)
+        base_cosines()
+        regroup_w(2, nc.scalar.copy)
+        nc.scalar.activation(out=unused[:], in_=eps[:], func=ACT.Abs_reciprocal_sqrt)
         quantise(0)
-        nc.vector.quantize_mx(
-            out=w_codes[:, 2 * E : 3 * E].bitcast(FP8X4), scales=w_scales[:, 2 * E : 3 * E],
-            in_=w_grouped[:, 2 * E * 4 : 3 * E * 4],
-        )
-        spread = ps_v.tile([P, SUB, E], F32, tag="av")
+        quantise_w(0, 2)
+        quantise_w(2, 3)
+        project_qk(0)
+        spread = ps_t.tile([P, SUB, E], F32, tag="tm")
         nc.tensor.matmul(
             out=spread[:, 0:2, :].rearrange("p s c -> p (s c)"), lhsT=ones[:],
             rhs=vectors[:, 2 * E : 4 * E], start=True, stop=True,
@@ -425,87 +441,85 @@ def tile_causalselfattention_pa_t_kernel(
                 out=spread[:, 2, 4 * t : 4 * t + 4], lhsT=vectors[:, t * E : (t + 1) * E],
                 rhs=ones[:, 0:4], start=True, stop=True,
             )
+        project_v(0)
+        regroup(1, 0, nc.scalar.copy)
+        turn(1, 1)
         bias_qk = const.tile([P, 2], F32)
         nc.vector.tensor_copy(out=bias_qk[:], in_=spread[:, 2, 0:8:4])
-        bias_v = const.tile([P, E], F32)
-        nc.vector.tensor_copy(out=bias_v[:], in_=spread[:, 0, :])
+        add_bias(0)
         gain = const.tile([P, 2, PAIRS, 2], F32)
         nc.vector.tensor_copy(
             out=gain[:].rearrange("p t j e -> p (t j e)"), in_=spread[:, 1, 0 : 2 * C]
         )
+        bias_v = const.tile([P, E], F32)
+        nc.vector.tensor_copy(out=bias_v[:], in_=spread[:, 0, :])
         signed = const.tile([P, 2, PAIRS, 2], F32)
         nc.vector.tensor_scalar_mul(out=signed[:, :, :, 0], in0=gain[:, :, :, 1], scalar1=-1.0)
         nc.vector.tensor_copy(out=signed[:, :, :, 1], in_=gain[:, :, :, 0])
-        mix_cosine = const.tile([P, 2, ROWS, PAIRS, 2], F32)
-        mix_sine = const.tile([P, 2, ROWS, PAIRS, 2], F32)
-        for mix, factor in ((mix_sine, signed), (mix_cosine, gain)):
-            for t in range(2):
-                nc.gpsimd.tensor_mul(
-                    out=mix[:, t, :, :, :],
-                    in0=hot[:].unsqueeze(3).to_broadcast([P, ROWS, PAIRS, 2]),
-                    in1=factor[:, t, :, :].unsqueeze(1).to_broadcast([P, ROWS, PAIRS, 2]),
-                )
-
-        chunk_turns()
+        regroup(1, 1, nc.vector.tensor_copy)
+        nc.vector.tensor_scalar_mul(out=minus_sine[:], in0=base[:, 0, P:], scalar1=-1.0)
+        quantise(1)
+        mix = const.tile([P, 2, 2, 2, SUB, C], F32)
+        for half in range(2):
+            for wave, factor in enumerate((signed, gain)):
+                for t in range(2):
+                    nc.gpsimd.tensor_mul(
+                        out=mix[:, wave, half, t, :, :].rearrange("p s (j e) -> p s j e", e=2),
+                        in0=hot[:, half * SUB : (half + 1) * SUB, :].unsqueeze(3)
+                        .to_broadcast([P, SUB, PAIRS, 2]),
+                        in1=factor[:, t, :, :].unsqueeze(1).to_broadcast([P, SUB, PAIRS, 2]),
+                    )
 
         def live(i):
             return 0 <= i < UNITS
 
-        both = slice(0, 2)
         LAST = UNITS - 1
-        for n in range(1, UNITS + 3):
-            roped = live(n - 4) and n - 4 < LAST - 1
-            if roped:
-                for t in range(2):
-                    times_sine(n - 4, t, nc.gpsimd)
-            if live(n - 2):
-                turn_back(n - 2, 0)
-            if live(n - 1) and n > 1:
-                quantise(n - 1)
-            if live(n - 3):
-                normalise(n - 3, 0)
-            if live(n - 1):
-                project_qk(n - 1)
-            if live(n - 2):
-                measure(n - 2, 0)
-            if n == 2:
-                cosines()
-                nc.scalar.activation(out=unused[:], in_=eps[:], func=ACT.Abs_reciprocal_sqrt)
-            if live(n - 2):
-                turn_back(n - 2, 1)
-                finish_v(n - 2)
-            if live(n - 1):
-                project_v(n - 1)
-            if live(n - 2):
-                measure(n - 2, 1)
-            if live(n - 1):
-                add_bias(n - 1)
-            if live(n - 2):
-                invert(n - 2)
-            if live(n):
-                turn(n)
-            if roped:
-                times_cosine(n - 4, both)
-            if live(n - 3):
-                normalise(n - 3, 1)
-            if roped:
-                finish_qk(n - 4, both)
-            if live(n - 2):
-                offset(n - 2)
-            if live(n):
-                regroup(n)
-            if n == 1:
-                sines()
-            if n % 2 == 0 and n // 2 - 1 < CHUNKS:
-                sine_table(n // 2 - 1)
-            if n % 2 == 1 and n >= 3 and (n - 3) // 2 < CHUNKS:
-                cosine_table((n - 3) // 2)
-            if n > LAST:
-                last = n - 3
-                if last >= LAST - 1:
-                    for t in range(2):
-                        times_cosine(last, slice(t, t + 1))
-                    times_sine(last, 0, nc.gpsimd)
-                    times_sine(last, 1, nc.vector)
-                    for t in range(2):
-                        finish_qk(last, slice(t, t + 1))
+        for n in range(2, UNITS + 3):
+            new, coded, measured, roped = n, n - 1, n - 2, n - 3
+            if live(measured):
+                turn_back(measured, 0)
+            if live(coded) and n > 2:
+                quantise(coded)
+            if live(roped):
+                normalise(roped, 0)
+            if live(measured):
+                turn_back(measured, 1)
+            if live(roped):
+                sine_copy(roped)
+                times_sine(roped, 0, nc.gpsimd)
+                normalise(roped, 1)
+                times_sine(roped, 1, nc.gpsimd if roped < LAST else nc.vector)
+            if live(coded):
+                project_qk(coded)
+                add_bias(coded)
+            if live(measured):
+                finish_v(measured)
+            if live(roped):
+                times_cosine(roped, 1)
+            if live(new):
+                turn(new, 0)
+            if live(measured):
+                measure(measured, 0)
+            if live(coded):
+                project_v(coded)
+            if live(measured):
+                sine_product(measured)
+                measure(measured, 1)
+            if live(new):
+                turn(new, 1)
+                regroup(new, 0, nc.scalar.copy)
+            if live(measured):
+                invert(measured)
+            if live(roped):
+                times_cosine(roped, 0)
+            if live(measured):
+                offset(measured)
+            if live(roped):
+                finish_qk(roped, 1)
+                finish_qk(roped, 0)
+            if live(measured):
+                cosine_product(measured)
+            if live(new):
+                regroup(new, 1, nc.scalar.copy)
+            if n <= CHUNKS:
+                turn_waves(n - 1)

@@ -82,12 +82,14 @@ def tile_causalselfattention_pa_t_kernel(
         def tokens_of(i):
             return slice((i // 2) * CHUNK, (i // 2 + 1) * CHUNK)
 
-        def load(i):
+        def load(i, pieces=1):
             x_rows[i] = xpool.tile([P, SUB, D], BF16, name="x_rows")
-            nc.sync.dma_start(
-                out=x_rows[i][:],
-                in_=x[tokens_of(i), :].rearrange("(p r) k -> p r k", r=ROWS)[:, rows_of(i), :],
-            )
+            rows = x[tokens_of(i), :].rearrange("(p r) k -> p r k", r=ROWS)[:, rows_of(i), :]
+            step = SUB // pieces
+            for s in range(0, SUB, step):
+                nc.sync.dma_start(
+                    out=x_rows[i][:, s : s + step, :], in_=rows[:, s : s + step, :]
+                )
 
         def store(dest, i, tile):
             nc.sync.dma_start(
@@ -97,7 +99,7 @@ def tile_causalselfattention_pa_t_kernel(
                 in_=tile,
             )
 
-        load(0)
+        load(0, 2)
         w_rows = const.tile([P, 3, D], BF16)
         nc.sync.dma_start(out=w_rows[:], in_=W_attn.rearrange("(a p) k -> p a k", p=P))
         vectors = const.tile([P, 4 * E], BF16)
@@ -203,6 +205,7 @@ def tile_causalselfattention_pa_t_kernel(
         quarter = const.tile([P, P + CHUNKS], F32)
         base = const.tile([P, 2, P + CHUNKS], F32)
         minus_sine = const.tile([P, CHUNKS], F32)
+        scaled = {}
         trig = {0: base}
 
         def base_sines():
@@ -218,17 +221,19 @@ def tile_causalselfattention_pa_t_kernel(
         def base_cosines():
             nc.scalar.activation(out=base[:, 1, :], in_=quarter[:], func=ACT.Sin, scale=2.0 * PI)
 
-        def turn_waves(b):
-            scaled = two.tile([P, 2, P], F32)
+        def scale_waves(b):
+            scaled[b] = const.tile([P, 2, P], F32, name="scaled" + str(b))
             nc.scalar.activation(
-                out=scaled[:], in_=base[:, :, 0:P], func=ACT.Copy,
+                out=scaled[b][:], in_=base[:, :, 0:P], func=ACT.Copy,
                 scale=base[:, 1, P + b : P + b + 1],
             )
+
+        def cross_waves(b):
             trig[b] = const.tile([P, 2, P], F32, name="trig" + str(b))
             for wave, factor in ((0, base[:, 0, P + b : P + b + 1]), (1, minus_sine[:, b : b + 1])):
                 nc.vector.scalar_tensor_tensor(
                     out=trig[b][:, wave, :], in0=base[:, 1 - wave, 0:P], scalar=factor,
-                    in1=scaled[:, wave, :], op0=ALU.mult, op1=ALU.add,
+                    in1=scaled[b][:, wave, :], op0=ALU.mult, op1=ALU.add,
                 )
 
         def turn(i, b):
@@ -364,9 +369,9 @@ def tile_causalselfattention_pa_t_kernel(
                 .unsqueeze(1).to_broadcast([P, H, SUB * C]),
             )
 
-        def finish_qk(i, t):
+        def finish_qk(i, t, engine):
             qk_out = three.tile([P, H, SUB, C], F32, name="qk_out" + str(t))
-            nc.vector.tensor_add(out=qk_out[:], in0=straight[i, t][:], in1=crossed[i, t][:])
+            engine.tensor_add(out=qk_out[:], in0=straight[i, t][:], in1=crossed[i, t][:])
             store((out_0, out_1)[t], i, qk_out[:])
 
         def gained(out, i, wave):
@@ -418,20 +423,7 @@ def tile_causalselfattention_pa_t_kernel(
             turn(0, b)
         for a in range(3):
             turn_w(a)
-        turn(1, 0)
-        regroup(0, 0, nc.scalar.copy)
-        regroup(0, 1, nc.vector.tensor_copy)
-        base_sines()
-        regroup_w(0, nc.scalar.copy)
-        regroup_w(1, nc.vector.tensor_copy)
-        base_cosines()
-        regroup_w(2, nc.scalar.copy)
-        nc.scalar.activation(out=unused[:], in_=eps[:], func=ACT.Abs_reciprocal_sqrt)
-        quantise(0)
-        quantise_w(0, 2)
-        quantise_w(2, 3)
-        project_qk(0)
-        spread = ps_t.tile([P, SUB, E], F32, tag="tm")
+        spread = ps_cos.tile([P, SUB, E], F32, tag="cosine")
         nc.tensor.matmul(
             out=spread[:, 0:2, :].rearrange("p s c -> p (s c)"), lhsT=ones[:],
             rhs=vectors[:, 2 * E : 4 * E], start=True, stop=True,
@@ -441,11 +433,24 @@ def tile_causalselfattention_pa_t_kernel(
                 out=spread[:, 2, 4 * t : 4 * t + 4], lhsT=vectors[:, t * E : (t + 1) * E],
                 rhs=ones[:, 0:4], start=True, stop=True,
             )
+        turn(1, 0)
+        regroup(0, 0, nc.scalar.copy)
+        regroup(0, 1, nc.vector.tensor_copy)
+        base_sines()
+        regroup_w(0, nc.scalar.copy)
+        regroup_w(1, nc.vector.tensor_copy)
+        base_cosines()
+        regroup_w(2, nc.scalar.copy)
+        nc.scalar.activation(out=unused[:], in_=eps[:], func=ACT.Abs_reciprocal_sqrt)
+        bias_qk = const.tile([P, 2], F32)
+        nc.vector.tensor_copy(out=bias_qk[:], in_=spread[:, 2, 0:8:4])
+        quantise(0)
+        quantise_w(0, 2)
+        quantise_w(2, 3)
+        project_qk(0)
         project_v(0)
         regroup(1, 0, nc.scalar.copy)
         turn(1, 1)
-        bias_qk = const.tile([P, 2], F32)
-        nc.vector.tensor_copy(out=bias_qk[:], in_=spread[:, 2, 0:8:4])
         add_bias(0)
         gain = const.tile([P, 2, PAIRS, 2], F32)
         nc.vector.tensor_copy(
@@ -487,39 +492,57 @@ def tile_causalselfattention_pa_t_kernel(
             if live(roped):
                 sine_copy(roped)
                 times_sine(roped, 0, nc.gpsimd)
+            if roped == LAST:
+                times_cosine(roped, 0)
+            if live(roped):
                 normalise(roped, 1)
-                times_sine(roped, 1, nc.gpsimd if roped < LAST else nc.vector)
+            if live(roped) and roped < LAST:
+                times_sine(roped, 1, nc.gpsimd)
+            if roped == LAST:
+                times_sine(roped, 1, nc.vector)
             if live(coded):
                 project_qk(coded)
+            if n == 2:
+                for b in range(1, CHUNKS - 1):
+                    scale_waves(b)
+            if n == 3:
+                scale_waves(CHUNKS - 1)
+            if live(coded):
                 add_bias(coded)
             if live(measured):
                 finish_v(measured)
+            if live(coded):
+                project_v(coded)
+            if live(measured):
+                measure(measured, 0)
             if live(roped):
                 times_cosine(roped, 1)
             if live(new):
                 turn(new, 0)
-            if live(measured):
-                measure(measured, 0)
-            if live(coded):
-                project_v(coded)
-            if live(measured):
-                sine_product(measured)
-                measure(measured, 1)
-            if live(new):
                 turn(new, 1)
+            if live(measured):
+                measure(measured, 1)
+                sine_product(measured)
+            if live(new):
                 regroup(new, 0, nc.scalar.copy)
             if live(measured):
                 invert(measured)
-            if live(roped):
+            if n == 2:
+                for b in range(1, CHUNKS - 1):
+                    cross_waves(b)
+            if n == 3:
+                cross_waves(CHUNKS - 1)
+            if live(roped) and roped < LAST:
                 times_cosine(roped, 0)
             if live(measured):
                 offset(measured)
+            if roped == LAST:
+                finish_qk(roped, 0, nc.vector)
             if live(roped):
-                finish_qk(roped, 1)
-                finish_qk(roped, 0)
+                finish_qk(roped, 1, nc.vector)
+            if live(roped) and roped < LAST:
+                finish_qk(roped, 0, nc.vector)
             if live(measured):
                 cosine_product(measured)
             if live(new):
                 regroup(new, 1, nc.scalar.copy)
-            if n <= CHUNKS:
-                turn_waves(n - 1)

from contextlib import ExitStack

import concourse.mybir as mybir
from concourse.masks import make_identity

F32 = mybir.dt.float32
BF16 = mybir.dt.bfloat16
U32 = mybir.dt.uint32
U8 = mybir.dt.uint8
FP8X4 = mybir.dt.float8_e4m3fn_x4
ALU = mybir.AluOpType
ACT = mybir.ActivationFunctionType
AX = mybir.AxisListType

T, D, H, C = 8192, 512, 4, 32
E = H * C
EPS = 1e-6
BASE = 10000.0
PI = 3.141592653589793

P = 128
ROWS = 8
CHUNK = P * ROWS
CHUNKS = T // CHUNK
SUB = ROWS // 2
UNIT = P * SUB
UNITS = 2 * CHUNKS
PAIRS = C // 2
GROUPS = 2 * SUB * H
ROUND = 12582912.0

FLOPS = 2 * T * D * 3 * E


def split_frequency(pair):
    turns = BASE ** (-pair / PAIRS) / (2.0 * PI)
    scale = 1.0
    while turns * scale < 1024.0:
        scale = scale * 2.0
    high = round(turns * scale) / scale
    return high, turns - high


def tile_causalselfattention_pa_t_kernel(
    tc, x, W_attn, b_attn, q_ln_w, k_ln_w, out_0, out_1, out_2
):
    nc = tc.nc
    with ExitStack() as ctx:
        const = ctx.enter_context(tc.tile_pool(name="const", bufs=1))
        xpool = ctx.enter_context(tc.tile_pool(name="xpool", bufs=UNITS))
        one = ctx.enter_context(tc.tile_pool(name="one", bufs=1))
        two = ctx.enter_context(tc.tile_pool(name="two", bufs=2))
        three = ctx.enter_context(tc.tile_pool(name="three", bufs=3))
        ps_io = ctx.enter_context(tc.psum_pool(name="ps_io", bufs=3))
        ps_v = ctx.enter_context(tc.psum_pool(name="ps_v", bufs=1))
        ps_t = ctx.enter_context(tc.psum_pool(name="ps_t", bufs=3))
        ps_cos = ctx.enter_context(tc.psum_pool(name="ps_cos", bufs=1))
        ctx.enter_context(tc.manual_schedule())

        x_rows = {}
        x_turned = {}
        grouped = {}
        codes = {}
        scales = {}
        acc = {}
        acc_v = {}
        biased = {}
        u = {}
        stats = {}
        rstd = {}
        shift = {}
        normed = {}
        straight = {}
        crossed = {}
        cosine = {}
        sine_raw = {}
        sine = {}

        def rows_of(i):
            return slice(SUB * (i % 2), SUB * (i % 2) + SUB)

        def tokens_of(i):
            return slice((i // 2) * CHUNK, (i // 2 + 1) * CHUNK)

        def load(i, pieces=1):
            x_rows[i] = xpool.tile([P, SUB, D], BF16, name="x_rows")
            rows = x[tokens_of(i), :].rearrange("(p r) k -> p r k", r=ROWS)[:, rows_of(i), :]
            step = SUB // pieces
            for s in range(0, SUB, step):
                nc.sync.dma_start(
                    out=x_rows[i][:, s : s + step, :], in_=rows[:, s : s + step, :]
                )

        def store(dest, i, tile):
            nc.sync.dma_start(
                out=dest[:, tokens_of(i), :].rearrange("h (p r) c -> p h r c", r=ROWS)[
                    :, :, rows_of(i), :
                ],
                in_=tile,
            )

        load(0, 2)
        w_rows = const.tile([P, 3, D], BF16)
        nc.sync.dma_start(out=w_rows[:], in_=W_attn.rearrange("(a p) k -> p a k", p=P))
        vectors = const.tile([P, 4 * E], BF16)
        nc.vector.memset(vectors[:], 0.0)
        nc.sync.dma_start(out=vectors[0:1, 0 : 3 * E], in_=b_attn.rearrange("(o n) -> o n", o=1))
        nc.sync.dma_start(
            out=vectors[0:1, 3 * E : 3 * E + C], in_=q_ln_w.rearrange("(o n) -> o n", o=1)
        )
        nc.sync.dma_start(
            out=vectors[0:1, 3 * E + C : 3 * E + 2 * C], in_=k_ln_w.rearrange("(o n) -> o n", o=1)
        )
        for i in range(1, UNITS):
            load(i)
        zero = const.tile([P, 1], F32)
        nc.vector.memset(zero[:], 0.0)
        unused = const.tile([P, 1], F32)
        nc.scalar.activation(out=unused[:], in_=zero[:], func=ACT.Sin)
        ones = const.tile([P, P], BF16)
        nc.vector.memset(ones[:], 1.0)
        eps = const.tile([P, 1], F32)
        nc.vector.memset(eps[:], EPS)
        highs = const.tile([P, PAIRS], F32)
        for j in range(PAIRS):
            nc.vector.memset(highs[:, j : j + 1], split_frequency(j)[0])

        lane = const.tile([P, 1], F32)
        nc.gpsimd.iota(
            lane[:], pattern=[[1, 1]], base=0, channel_multiplier=1,
            allow_small_or_imprecise_dtypes=True,
        )
        slot = const.tile([P, ROWS, PAIRS], F32)
        nc.gpsimd.iota(
            slot[:], pattern=[[PAIRS, ROWS], [1, PAIRS]], base=0, channel_multiplier=0,
            allow_small_or_imprecise_dtypes=True,
        )
        slot_row = const.tile([P, ROWS, PAIRS], F32)
        nc.gpsimd.iota(
            slot_row[:], pattern=[[1, ROWS], [0, PAIRS]], base=0, channel_multiplier=0,
            allow_small_or_imprecise_dtypes=True,
        )
        first = const.tile([P, P], F32)
        nc.gpsimd.iota(
            first[:], pattern=[[ROWS, P]], base=0, channel_multiplier=0,
            allow_small_or_imprecise_dtypes=True,
        )
        token = const.tile([P, P + CHUNKS], F32)
        nc.gpsimd.iota(
            token[:, P:], pattern=[[CHUNK, CHUNKS]], base=0, channel_multiplier=0,
            allow_small_or_imprecise_dtypes=True,
        )
        ident = const.tile([P, P], F32)
        make_identity(nc, ident[:])
        hot = const.tile([P, ROWS, PAIRS], F32)
        nc.vector.tensor_scalar(
            out=hot[:], in0=slot[:], scalar1=lane[:, 0:1], scalar2=None, op0=ALU.is_equal
        )
        hot_pair = const.tile([P, PAIRS], F32)
        nc.vector.reduce_sum(
            out=hot_pair[:], in_=hot[:].rearrange("p r j -> p j r"), axis=AX.X
        )
        own_row = const.tile([P, ROWS, PAIRS], F32)
        nc.vector.tensor_mul(out=own_row[:], in0=hot[:], in1=slot_row[:])
        high_terms = const.tile([P, PAIRS], F32)
        nc.vector.tensor_mul(out=high_terms[:], in0=hot_pair[:], in1=highs[:])
        low_terms = const.tile([P, PAIRS], F32)
        for j in range(PAIRS):
            nc.scalar.mul(low_terms[:, j : j + 1], hot_pair[:, j : j + 1], split_frequency(j)[1])
        row = const.tile([P, 1], F32)
        nc.vector.reduce_sum(
            out=row[:], in_=own_row[:].rearrange("p r j -> p (r j)"), axis=AX.X
        )
        frequency = const.tile([P, 2], F32)
        nc.vector.reduce_sum(out=frequency[:, 0:1], in_=high_terms[:], axis=AX.X)

        def fraction(out, turns, scratch):
            nc.vector.tensor_scalar(
                out=scratch, in0=turns, scalar1=ROUND, scalar2=ROUND,
                op0=ALU.add, op1=ALU.subtract,
            )
            nc.vector.tensor_sub(out=out, in0=turns, in1=scratch)

        nc.vector.tensor_scalar(
            out=token[:, 0:P], in0=first[:], scalar1=row[:, 0:1], scalar2=None, op0=ALU.add
        )
        whole = const.tile([P, P + CHUNKS], F32)
        nc.vector.tensor_scalar(
            out=whole[:], in0=token[:], scalar1=frequency[:, 0:1], scalar2=ROUND,
            op0=ALU.mult, op1=ALU.add,
        )
        nc.vector.tensor_scalar_sub(out=whole[:], in0=whole[:], scalar1=ROUND)
        nc.vector.scalar_tensor_tensor(
            out=whole[:], in0=token[:], scalar=frequency[:, 0:1], in1=whole[:],
            op0=ALU.mult, op1=ALU.subtract,
        )
        nc.vector.reduce_sum(out=frequency[:, 1:2], in_=low_terms[:], axis=AX.X)
        nc.vector.scalar_tensor_tensor(
            out=whole[:], in0=token[:], scalar=frequency[:, 1:2], in1=whole[:],
            op0=ALU.mult, op1=ALU.add,
        )
        base_turns = const.tile([P, P + CHUNKS], F32)
        base_scratch = const.tile([P, P + CHUNKS], F32)
        fraction(base_turns[:], whole[:], base_scratch[:])
        quarter = const.tile([P, P + CHUNKS], F32)
        base = const.tile([P, 2, P + CHUNKS], F32)
        minus_sine = const.tile([P, CHUNKS], F32)
        scaled = {}
        trig = {0: base}

        def base_sines():
            nc.scalar.activation(out=quarter[:], in_=base_turns[:], func=ACT.Abs)
            nc.scalar.activation(
                out=base[:, 0, :], in_=base_turns[:], func=ACT.Sin, scale=2.0 * PI
            )
            nc.vector.tensor_scalar(
                out=quarter[:], in0=quarter[:], scalar1=-1.0, scalar2=0.25,
                op0=ALU.mult, op1=ALU.add,
            )

        def base_cosines():
            nc.scalar.activation(out=base[:, 1, :], in_=quarter[:], func=ACT.Sin, scale=2.0 * PI)

        def scale_waves(b):
            scaled[b] = const.tile([P, 2, P], F32, name="scaled" + str(b))
            nc.scalar.activation(
                out=scaled[b][:], in_=base[:, :, 0:P], func=ACT.Copy,
                scale=base[:, 1, P + b : P + b + 1],
            )

        def cross_waves(b):
            trig[b] = const.tile([P, 2, P], F32, name="trig" + str(b))
            for wave, factor in ((0, base[:, 0, P + b : P + b + 1]), (1, minus_sine[:, b : b + 1])):
                nc.vector.scalar_tensor_tensor(
                    out=trig[b][:, wave, :], in0=base[:, 1 - wave, 0:P], scalar=factor,
                    in1=scaled[b][:, wave, :], op0=ALU.mult, op1=ALU.add,
                )

        def turn(i, b):
            xt = ps_io.tile([P, 2, 2, P], F32, tag="io")
            for s in range(2):
                for half in range(2):
                    nc.tensor.transpose(
                        xt[:, s, half, :],
                        x_rows[i][:, 2 * b + s, :].bitcast(F32)[:, half : 2 * P : 2],
                        ident[:],
                    )
            x_turned[i, b] = xt

        def regroup(i, b, copy):
            if b == 0:
                grouped[i] = two.tile([P, UNIT * 4], BF16, align_bytes=64, name="grouped")
            words = grouped[i][:].bitcast(F32).rearrange("p (s m e) -> p s m e", s=SUB, e=2)
            copy(
                out=words[:, 2 * b : 2 * b + 2, :, :],
                in_=x_turned[i, b][:].rearrange("p s e m -> p s m e"),
            )

        def quantise(i):
            codes[i] = two.tile([P, UNIT], U32, align_bytes=64, name="codes")
            scales[i] = two.tile([P, UNIT], U8, align_bytes=64, name="scales")
            nc.vector.quantize_mx(
                out=codes[i][:].bitcast(FP8X4), scales=scales[i][:], in_=grouped[i][:]
            )

        def project_qk(i):
            acc[i] = []
            for t in range(2):
                cm = ps_io.tile([P, UNIT], F32, tag="io")
                nc.tensor.matmul_mx(
                    out=cm[:],
                    lhsT=w_codes[:, t * E : (t + 1) * E].bitcast(FP8X4),
                    lhsT_scale=w_scales[:, t * E : (t + 1) * E],
                    rhs=codes[i][:].bitcast(FP8X4), rhs_scale=scales[i][:],
                    start=True, stop=True,
                )
                acc[i].append(cm)

        def project_v(i):
            acc_v[i] = ps_v.tile([P, SUB, E], F32, tag="av", name="acc_v")
            for s in range(SUB):
                cols = slice(s * P, (s + 1) * P)
                nc.tensor.matmul_mx(
                    out=acc_v[i][:, s, :],
                    lhsT=codes[i][:, cols].bitcast(FP8X4), lhsT_scale=scales[i][:, cols],
                    rhs=w_codes[:, 2 * E : 3 * E].bitcast(FP8X4),
                    rhs_scale=w_scales[:, 2 * E : 3 * E],
                    start=True, stop=True,
                )

        def add_bias(i):
            biased[i] = []
            for t in range(2):
                cb = two.tile([P, UNIT], F32, tag="cb" + str(t))
                nc.scalar.activation(
                    out=cb[:], in_=acc[i][t][:], func=ACT.Identity, bias=bias_qk[:, t : t + 1]
                )
                biased[i].append(cb)

        def turn_back(i, t):
            tm = ps_t.tile([P, SUB, E], F32, tag="tm")
            for s in range(SUB):
                nc.tensor.transpose(tm[:, s, :], biased[i][t][:, s * P : (s + 1) * P], ident[:])
            u[i, t] = tm

        def finish_v(i):
            v_out = three.tile([P, H, SUB, C], F32)
            nc.vector.tensor_add(
                out=v_out[:],
                in0=acc_v[i][:].rearrange("p s (h c) -> p h s c", c=C),
                in1=bias_v[:].rearrange("p (h c) -> p h c", c=C).unsqueeze(2)
                .to_broadcast([P, H, SUB, C]),
            )
            store(out_2, i, v_out[:])

        def measure(i, t):
            if t == 0:
                stats[i] = three.tile([P, GROUPS, 3], F32, name="stats")
            for s in range(SUB):
                for h in range(0, H, 2):
                    g = (t * SUB + s) * H + h
                    nc.vector.bn_stats(
                        out=stats[i][:, g : g + 2, :].rearrange("p two k -> p (two k)"),
                        in_=u[i, t][:, s, h * C : (h + 2) * C].rearrange(
                            "p (two c) -> p c two", two=2
                        ),
                    )

        def invert(i):
            rstd[i] = three.tile([P, GROUPS], F32, name="rstd")
            nc.scalar.activation(
                out=rstd[i][:], in_=stats[i][:, :, 2], func=ACT.Abs_reciprocal_sqrt,
                scale=1.0 / C, bias=eps[:],
            )

        def offset(i):
            shift[i] = three.tile([P, GROUPS], F32, name="shift")
            nc.vector.scalar_tensor_tensor(
                out=shift[i][:], in0=stats[i][:, :, 1], scalar=-1.0, in1=rstd[i][:],
                op0=ALU.mult, op1=ALU.mult,
            )

        def normalise(i, t):
            normed[i, t] = two.tile([P, H, SUB, C], F32, name="normed" + str(t))
            for s in range(SUB):
                for h in range(H):
                    g = (t * SUB + s) * H + h
                    nc.scalar.activation(
                        out=normed[i, t][:, h, s, :],
                        in_=u[i, t][:, s, h * C : (h + 1) * C], func=ACT.Identity,
                        scale=rstd[i][:, g : g + 1], bias=shift[i][:, g : g + 1],
                    )

        def times_sine(i, t, engine):
            crossed[i, t] = one.tile([P, H, SUB, C], F32, name="crossed" + str(t))
            engine.tensor_mul(
                out=crossed[i, t][:].rearrange("p h s (j e) -> p h (s j) e", e=2),
                in0=normed[i, t][:].rearrange("p h s (j e) -> p h (s j) e", e=2)[:, :, :, ::-1],
                in1=sine[i][:, t, :, :].rearrange("p s (j e) -> p (s j) e", e=2)
                .unsqueeze(1).to_broadcast([P, H, SUB * PAIRS, 2]),
            )

        def times_cosine(i, t):
            straight[i, t] = two.tile([P, H, SUB, C], F32, name="straight" + str(t))
            nc.vector.tensor_mul(
                out=straight[i, t][:].rearrange("p h s c -> p h (s c)"),
                in0=normed[i, t][:].rearrange("p h s c -> p h (s c)"),
                in1=cosine[i][:, t, :, :].rearrange("p s c -> p (s c)")
                .unsqueeze(1).to_broadcast([P, H, SUB * C]),
            )

        def finish_qk(i, t, engine):
            qk_out = three.tile([P, H, SUB, C], F32, name="qk_out" + str(t))
            engine.tensor_add(out=qk_out[:], in0=straight[i, t][:], in1=crossed[i, t][:])
            store((out_0, out_1)[t], i, qk_out[:])

        def gained(out, i, wave):
            nc.tensor.matmul(
                out=out.rearrange("p t s c -> p (t s c)"), lhsT=trig[i // 2][:, wave, 0:P],
                rhs=mix[:, wave, i % 2, :, :, :].rearrange("p t s c -> p (t s c)"),
                start=True, stop=True,
            )

        def sine_product(i):
            sine_raw[i] = ps_io.tile([P, 2, SUB, C], F32, tag="io", name="sine_raw")
            gained(sine_raw[i][:], i, 0)

        def sine_copy(i):
            sine[i] = two.tile([P, 2, SUB, C], F32, name="sine")
            nc.scalar.copy(out=sine[i][:], in_=sine_raw[i][:])

        def cosine_product(i):
            cosine[i] = ps_cos.tile([P, 2, SUB, C], F32, tag="cosine", name="cosine")
            gained(cosine[i][:], i, 1)

        w_grouped = const.tile([P, 3 * E * 4], BF16, align_bytes=64)
        w_words = w_grouped[:].bitcast(F32).rearrange("p (a r e) -> p a r e", a=3, e=2)
        w_codes = const.tile([P, 3 * E], U32, align_bytes=64)
        w_scales = const.tile([P, 3 * E], U8, align_bytes=64)
        w_turned = []

        def quantise_w(a, b):
            nc.vector.quantize_mx(
                out=w_codes[:, a * E : b * E].bitcast(FP8X4), scales=w_scales[:, a * E : b * E],
                in_=w_grouped[:, a * E * 4 : b * E * 4],
            )

        def turn_w(a):
            wt = ps_t.tile([P, SUB, E], F32, tag="tm")
            for half in range(2):
                nc.tensor.transpose(
                    wt[:, half, :], w_rows[:, a, :].bitcast(F32)[:, half : 2 * P : 2], ident[:]
                )
            w_turned.append(wt)

        def regroup_w(a, copy):
            copy(
                out=w_words[:, a, :, :],
                in_=w_turned[a][:, 0:2, :].rearrange("p e r -> p r e"),
            )

        for b in range(2):
            turn(0, b)
        for a in range(3):
            turn_w(a)
        spread = ps_cos.tile([P, SUB, E], F32, tag="cosine")
        nc.tensor.matmul(
            out=spread[:, 0:2, :].rearrange("p s c -> p (s c)"), lhsT=ones[:],
            rhs=vectors[:, 2 * E : 4 * E], start=True, stop=True,
        )
        for t in range(2):
            nc.tensor.matmul(
                out=spread[:, 2, 4 * t : 4 * t + 4], lhsT=vectors[:, t * E : (t + 1) * E],
                rhs=ones[:, 0:4], start=True, stop=True,
            )
        turn(1, 0)
        regroup(0, 0, nc.scalar.copy)
        regroup(0, 1, nc.vector.tensor_copy)
        base_sines()
        regroup_w(0, nc.scalar.copy)
        regroup_w(1, nc.vector.tensor_copy)
        base_cosines()
        regroup_w(2, nc.scalar.copy)
        nc.scalar.activation(out=unused[:], in_=eps[:], func=ACT.Abs_reciprocal_sqrt)
        bias_qk = const.tile([P, 2], F32)
        nc.vector.tensor_copy(out=bias_qk[:], in_=spread[:, 2, 0:8:4])
        quantise(0)
        quantise_w(0, 2)
        quantise_w(2, 3)
        project_qk(0)
        project_v(0)
        regroup(1, 0, nc.scalar.copy)
        turn(1, 1)
        add_bias(0)
        gain = const.tile([P, 2, PAIRS, 2], F32)
        nc.vector.tensor_copy(
            out=gain[:].rearrange("p t j e -> p (t j e)"), in_=spread[:, 1, 0 : 2 * C]
        )
        bias_v = const.tile([P, E], F32)
        nc.vector.tensor_copy(out=bias_v[:], in_=spread[:, 0, :])
        signed = const.tile([P, 2, PAIRS, 2], F32)
        nc.vector.tensor_scalar_mul(out=signed[:, :, :, 0], in0=gain[:, :, :, 1], scalar1=-1.0)
        nc.vector.tensor_copy(out=signed[:, :, :, 1], in_=gain[:, :, :, 0])
        regroup(1, 1, nc.vector.tensor_copy)
        nc.vector.tensor_scalar_mul(out=minus_sine[:], in0=base[:, 0, P:], scalar1=-1.0)
        quantise(1)
        mix = const.tile([P, 2, 2, 2, SUB, C], F32)
        for half in range(2):
            for wave, factor in enumerate((signed, gain)):
                for t in range(2):
                    nc.gpsimd.tensor_mul(
                        out=mix[:, wave, half, t, :, :].rearrange("p s (j e) -> p s j e", e=2),
                        in0=hot[:, half * SUB : (half + 1) * SUB, :].unsqueeze(3)
                        .to_broadcast([P, SUB, PAIRS, 2]),
                        in1=factor[:, t, :, :].unsqueeze(1).to_broadcast([P, SUB, PAIRS, 2]),
                    )

        def live(i):
            return 0 <= i < UNITS

        LAST = UNITS - 1
        for n in range(2, UNITS + 3):
            new, coded, measured, roped = n, n - 1, n - 2, n - 3
            if live(measured):
                turn_back(measured, 0)
            if live(coded) and n > 2:
                quantise(coded)
            if live(roped):
                normalise(roped, 0)
            if live(measured):
                turn_back(measured, 1)
            if live(roped):
                sine_copy(roped)
                times_sine(roped, 0, nc.gpsimd)
            if roped == LAST:
                times_cosine(roped, 0)
            if live(roped):
                normalise(roped, 1)
            if live(roped) and roped < LAST:
                times_sine(roped, 1, nc.gpsimd)
            if roped == LAST:
                times_sine(roped, 1, nc.vector)
            if live(coded):
                project_qk(coded)
            if n == 2:
                for b in range(1, CHUNKS - 1):
                    scale_waves(b)
            if n == 3:
                scale_waves(CHUNKS - 1)
            if live(coded):
                add_bias(coded)
            if live(measured):
                finish_v(measured)
            if live(coded):
                project_v(coded)
            if live(measured):
                measure(measured, 0)
            if live(roped):
                times_cosine(roped, 1)
            if live(new):
                turn(new, 0)
                turn(new, 1)
            if live(measured):
                measure(measured, 1)
                sine_product(measured)
            if live(new):
                regroup(new, 0, nc.scalar.copy)
            if live(measured):
                invert(measured)
            if n == 2:
                for b in range(1, CHUNKS - 1):
                    cross_waves(b)
            if n == 3:
                cross_waves(CHUNKS - 1)
            if live(roped) and roped < LAST:
                times_cosine(roped, 0)
            if live(measured):
                offset(measured)
            if roped == LAST:
                finish_qk(roped, 0, nc.vector)
            if live(roped):
                finish_qk(roped, 1, nc.vector)
            if live(roped) and roped < LAST:
                finish_qk(roped, 0, nc.vector)
            if live(measured):
                cosine_product(measured)
            if live(new):
                regroup(new, 1, nc.scalar.copy)
